import numpy as np
import ml_dtypes


def mxq(x, axis, fmt="e4m3"):
    dtype, down = {"e4m3": (ml_dtypes.float8_e4m3fn, 7), "e5m2": (ml_dtypes.float8_e5m2, 14)}[fmt]
    v = np.moveaxis(np.asarray(x, np.float32).astype(ml_dtypes.bfloat16).astype(np.float64), axis, -1)
    blocks = v.reshape(v.shape[:-1] + (-1, 32))
    amax = np.abs(blocks).max(-1, keepdims=True)
    byte = np.maximum(np.where(amax > 0, np.frexp(amax)[1] - 1 + 127, 0) - down, 1)
    scale = np.exp2(byte - 127.0)
    codes = (blocks / scale).astype(np.float32).astype(dtype).astype(np.float64)
    return np.moveaxis((codes * scale).reshape(v.shape), -1, axis)


WIDE = False


def mx_kscale(k):
    if not WIDE:
        return np.ones(k)
    levels = np.array([10, -10, 5, -5, 0])
    a = np.random.permutation(np.resize(levels, k // 512 * 4)).reshape(k // 512, 4)
    idx = np.arange(k)
    return np.exp2(a[idx // 512, idx % 128 // 32])


BF16 = ml_dtypes.bfloat16


def bf(x):
    return np.asarray(x, np.float32).astype(BF16)


def f64(x):
    return np.asarray(x).astype(np.float64)


E2M1 = np.array([0.0, 0.5, 1.0, 1.5, 2.0, 3.0, 4.0, 6.0, -0.0, -0.5, -1.0, -1.5, -2.0, -3.0, -4.0, -6.0])


def pack_weight(w, fmt):
    k, n = w.shape
    w = f64(bf(w)).reshape(k // 32, 32, n)
    amax = np.abs(w).max(1)
    if fmt == "e4m3":
        byte = np.frexp(amax)[1] - 1 + 127 - 7
    else:
        mant, ex = np.frexp(amax / 6.0)
        byte = np.where(mant > 0.5, ex, ex - 1) + 127
    byte = np.clip(np.where(amax > 0, byte, 1), 1, 254)
    scaled = (w * np.exp2(127.0 - byte)[:, None, :]).reshape(k, n).astype(np.float32)
    by_word = np.ascontiguousarray(scaled.reshape(k // 512, 128, 4, n).transpose(0, 1, 3, 2))
    if fmt == "e4m3":
        words = by_word.astype(ml_dtypes.float8_e4m3fn).view(np.uint8)
    else:
        c = by_word.astype(ml_dtypes.float4_e2m1fn).view(np.uint8) & 0xF
        words = c[..., 0::2] | (c[..., 1::2] << 4)
    return np.ascontiguousarray(words), np.ascontiguousarray(byte.astype(np.uint8).reshape(k // 512, 16, n))


def unpack_weight(words, scales, fmt):
    g, p, n, _ = words.shape
    if fmt == "e4m3":
        vals = np.ascontiguousarray(words).view(ml_dtypes.float8_e4m3fn).astype(np.float64)
    else:
        nib = np.empty((g, p, n, 4), np.uint8)
        nib[..., 0::2] = words & 0xF
        nib[..., 1::2] = words >> 4
        vals = E2M1[nib]
    vals = vals * np.repeat(np.exp2(scales.astype(np.float64) - 127.0), 8, axis=1)[..., None]
    return vals.transpose(0, 1, 3, 2).reshape(g * 512, n)


B, IN, H = 512, 512, 1024
D = IN + H
LN_EPS = 1e-5
DIV_EPS = 1e-6


def sigmoid(v):
    return 1.0 / (1.0 + np.exp(-v))


def setup_inputs():
    s = mx_kscale(D)
    d = {"x": bf(np.random.standard_normal((B, IN)) * s[:IN]),
         "h_prev": bf(np.random.standard_normal((B, H)) * s[IN:]),
         "c_prev": bf(np.random.standard_normal((B, H))),
         "n_prev": bf(np.random.uniform(0.0, 1.0, (B, H))),
         "m_prev": bf(np.random.uniform(0.0, 1.0, (B, H)))}
    for g in "ifoz":
        w = np.random.standard_normal((H, D)) * 0.6 / np.sqrt(D) / s
        words, scales = pack_weight(np.ascontiguousarray(w.T), "e4m3")
        d["W" + g + "_words"] = words
        d["W" + g + "_scales"] = scales
        d["b" + g] = bf(np.random.standard_normal(H) * 0.3)
    d["ln_gamma"] = bf(1.0 + 0.1 * np.random.standard_normal(H))
    d["ln_beta"] = bf(0.1 * np.random.standard_normal(H))
    return d


def reference(x, h_prev, c_prev, n_prev, m_prev, Wi_words, Wi_scales, bi, Wf_words, Wf_scales, bf, Wo_words, Wo_scales, bo, Wz_words, Wz_scales, bz, ln_gamma, ln_beta):
    combined = np.concatenate([f64(x), f64(h_prev)], axis=1)
    Wt = np.stack([unpack_weight(Wi_words, Wi_scales, "e4m3"),
                   unpack_weight(Wf_words, Wf_scales, "e4m3"),
                   unpack_weight(Wo_words, Wo_scales, "e4m3"),
                   unpack_weight(Wz_words, Wz_scales, "e4m3")], axis=0)
    b = np.stack([f64(bi), f64(bf), f64(bo), f64(bz)], axis=0)
    gates = (mxq(combined, 1, "e4m3") @ Wt) + b[:, None, :]
    i_t = np.exp(gates[0])
    f_t = sigmoid(gates[1])
    o_t = sigmoid(gates[2])
    z_t = np.tanh(gates[3])
    c_t = f_t * f64(c_prev) + i_t * z_t
    n_t = f_t * f64(n_prev) + i_t
    m_t = np.maximum(f_t * f64(m_prev), np.abs(i_t * z_t))
    h = o_t * (c_t / (n_t + DIV_EPS))
    mu = np.mean(h, axis=-1, keepdims=True)
    var = np.mean(np.square(h - mu), axis=-1, keepdims=True)
    h_t = (h - mu) * (1.0 / np.sqrt(var + LN_EPS)) * f64(ln_gamma) + f64(ln_beta)
    return (h_t, c_t, n_t, m_t)

@@ -1,0 +1,355 @@
+from contextlib import ExitStack
+
+import concourse.mybir as mybir
+from concourse.masks import make_identity
+
+F32 = mybir.dt.float32
+BF16 = mybir.dt.bfloat16
+I32 = mybir.dt.int32
+U32 = mybir.dt.uint32
+U8 = mybir.dt.uint8
+FP8X4 = mybir.dt.float8_e4m3fn_x4
+ACT = mybir.ActivationFunctionType
+ALU = mybir.AluOpType
+
+P = 128
+B, IN, H = 512, 512, 1024
+D = IN + H
+K_PASS = 4 * P
+PASSES = D // K_PASS
+LN_EPS = 1e-5
+DIV_EPS = 1e-6
+
+ROW_TILES = B // P
+HALVES = 2
+HALF_TILES = ROW_TILES // HALVES
+HALF_B = B // HALVES
+PAIR_F = 2 * P
+PAIRS = H // PAIR_F
+BN_CHUNK = 512
+
+GATES = ("i", "z", "f", "o")
+UNITS = HALVES * PAIRS
+
+FLOPS = 2 * B * D * 4 * H
+
+
+def tile_slstmcell_kernel(
+    tc,
+    x,
+    h_prev,
+    c_prev,
+    n_prev,
+    m_prev,
+    Wi_words,
+    Wi_scales,
+    bi,
+    Wf_words,
+    Wf_scales,
+    bf,
+    Wo_words,
+    Wo_scales,
+    bo,
+    Wz_words,
+    Wz_scales,
+    bz,
+    ln_gamma,
+    ln_beta,
+    out_0,
+    out_1,
+    out_2,
+    out_3,
+):
+    nc = tc.nc
+    words_in = {"i": Wi_words, "z": Wz_words, "f": Wf_words, "o": Wo_words}
+    scales_in = {"i": Wi_scales, "z": Wz_scales, "f": Wf_scales, "o": Wo_scales}
+    bias_in = {"i": bi, "z": bz, "f": bf, "o": bo}
+    gate_func = {"i": ACT.Exp, "z": ACT.Tanh, "f": ACT.Tanh, "o": ACT.Tanh}
+    gate_scale = {"i": 1.0, "z": 1.0, "f": 0.5, "o": 0.5}
+
+    def by_row_tile(dram):
+        return dram.rearrange("(t p) f -> p t f", p=P)
+
+    with ExitStack() as ctx:
+        ctx.enter_context(tc.manual_schedule())
+        keep = ctx.enter_context(tc.tile_pool(name="keep", bufs=1))
+        gate_psum = ctx.enter_context(tc.psum_pool(name="gate_psum", bufs=4))
+        turn_psum = ctx.enter_context(tc.psum_pool(name="turn_psum", bufs=4))
+
+        planes = keep.tile([P, PASSES, H], U8, align_bytes=64)
+        nc.vector.memset(planes[:].rearrange("p g n -> p (g n)").bitcast(I32), 0)
+        ident = keep.tile([P, P], F32)
+        make_identity(nc, ident[:])
+        div_eps = keep.tile([P, 1], F32)
+        minus_half = keep.tile([P, 1], F32)
+
+        w_words = {}
+        for gate in GATES:
+            w_words[gate] = keep.tile([P, PASSES, H], U32, name="w_words_" + gate, align_bytes=64)
+        old_n = keep.tile([P, ROW_TILES, H], BF16)
+        old_c = keep.tile([P, ROW_TILES, H], BF16)
+        old_m = keep.tile([P, ROW_TILES, H], BF16)
+        codes = keep.tile([P, PASSES, B], U32, align_bytes=64)
+        code_scales = keep.tile([P, PASSES, B], U8, align_bytes=64)
+        bias_cols = keep.tile([P, 8 * len(GATES)], F32)
+        gamma_all = keep.tile([P, H], BF16)
+        beta_all = keep.tile([P, H], BF16)
+
+        def load_weight_columns(pair):
+            cols = slice(pair * PAIR_F, (pair + 1) * PAIR_F)
+            for gate in GATES:
+                nc.sync.dma_start(
+                    out=w_words[gate][:, :, cols].bitcast(I32),
+                    in_=words_in[gate].rearrange("g p n t -> p g (n t)").bitcast(I32)[:, :, cols],
+                )
+
+        def load_old_state(half):
+            rows = slice(half * HALF_TILES, (half + 1) * HALF_TILES)
+            nc.sync.dma_start(out=old_m[:, rows, :], in_=by_row_tile(m_prev)[:, rows, :])
+            nc.sync.dma_start(out=old_c[:, rows, :], in_=by_row_tile(c_prev)[:, rows, :])
+            nc.sync.dma_start(out=old_n[:, rows, :], in_=by_row_tile(n_prev)[:, rows, :])
+
+        with tc.tile_pool(name="prep", bufs=1) as prep:
+            bias_rows = prep.tile([P, P], BF16)
+            nc.vector.memset(bias_rows[:], 0.0)
+            norm_rows = prep.tile([P, 2, H], BF16)
+            nc.vector.memset(norm_rows[:].rearrange("p v f -> p (v f)").bitcast(I32), 0)
+            ones = prep.tile([P, P], BF16)
+            nc.vector.memset(ones[:], 1.0)
+            nc.vector.memset(div_eps[:], DIV_EPS)
+            nc.vector.memset(minus_half[:], -0.5)
+
+            combined = prep.tile([P, ROW_TILES, D], BF16)
+            nc.sync.dma_start(out=combined[:, :, 0:IN], in_=by_row_tile(x))
+            nc.sync.dma_start(out=combined[:, :, IN:D], in_=by_row_tile(h_prev))
+            for a, gate in enumerate(GATES):
+                nc.scalar.dma_start(
+                    out=bias_rows[8 * a : 8 * a + 8, :],
+                    in_=bias_in[gate].rearrange("(j f) -> j f", f=P),
+                )
+            nc.scalar.dma_start(out=norm_rows[0:1, 0, :], in_=ln_gamma.rearrange("(o f) -> o f", o=1))
+            nc.scalar.dma_start(out=norm_rows[0:1, 1, :], in_=ln_beta.rearrange("(o f) -> o f", o=1))
+            for a, gate in enumerate(GATES):
+                for r in range(4):
+                    nc.sync.dma_start(
+                        out=planes[4 * a + r : P : 32, :, :].bitcast(I32),
+                        in_=scales_in[gate].rearrange("g (q r) n -> r q g n", r=4)[r].bitcast(I32),
+                    )
+            load_weight_columns(0)
+            load_old_state(0)
+            for pair in range(1, PAIRS):
+                load_weight_columns(pair)
+            load_old_state(1)
+
+            bias_rows_f32 = prep.tile([P, P], F32)
+            nc.vector.tensor_copy(out=bias_rows_f32[:], in_=bias_rows[:])
+            bias_turned = turn_psum.tile([P, P], F32, tag="turn")
+            nc.tensor.transpose(bias_turned[:], bias_rows_f32[:], ident[:])
+            nc.vector.tensor_copy(out=bias_cols[:, 0:16], in_=bias_turned[:, 0:16])
+            nc.vector.tensor_scalar_mul(out=bias_cols[:, 16:32], in0=bias_turned[:, 16:32], scalar1=0.5)
+
+            for half in range(HALVES):
+                grouped = {}
+                for g in range(PASSES):
+                    k_turned = turn_psum.tile([P, 2, HALF_B], F32, tag="turn")
+                    for tt in range(HALF_TILES):
+                        pairs_of_k = combined[:, half * HALF_TILES + tt, :].bitcast(F32)
+                        for u in range(2):
+                            nc.tensor.transpose(
+                                k_turned[:, u, tt * P : (tt + 1) * P],
+                                pairs_of_k[:, 256 * g + u : 256 * (g + 1) : 2],
+                                ident[:],
+                            )
+                    grouped[g] = prep.tile(
+                        [P, HALF_B, 4], BF16, name="grouped_%d_%d" % (half, g), align_bytes=64
+                    )
+                    copy_out = nc.vector.tensor_copy if g % 2 == 0 else nc.scalar.copy
+                    copy_out(
+                        out=grouped[g][:].bitcast(F32),
+                        in_=k_turned[:].rearrange("p u b -> p b u"),
+                    )
+                for g in range(PASSES):
+                    rows = slice(half * HALF_B, (half + 1) * HALF_B)
+                    nc.vector.quantize_mx(
+                        out=codes[:, g, rows].bitcast(FP8X4),
+                        scales=code_scales[:, g, rows],
+                        in_=grouped[g][:].rearrange("p b t -> p (b t)"),
+                    )
+
+            for v, spread in enumerate((gamma_all, beta_all)):
+                for c in range(H // BN_CHUNK):
+                    cols = slice(c * BN_CHUNK, (c + 1) * BN_CHUNK)
+                    summed = gate_psum.tile([P, BN_CHUNK], F32, tag="sums")
+                    nc.tensor.matmul(summed[:], lhsT=ones[:], rhs=norm_rows[:, v, cols], start=True, stop=True)
+                    nc.scalar.copy(out=spread[:, cols], in_=summed[:])
+
+        acts = ctx.enter_context(tc.tile_pool(name="acts", bufs=2))
+        work = ctx.enter_context(tc.tile_pool(name="work", bufs=2))
+        halves = ctx.enter_context(tc.tile_pool(name="halves", bufs=HALVES))
+        small = ctx.enter_context(tc.tile_pool(name="small", bufs=ROW_TILES))
+
+        new_n, new_c, new_m, hidden, recip = {}, {}, {}, {}, {}
+        for half in range(HALVES):
+            new_n[half] = halves.tile([P, HALF_TILES, H], F32, name="new_n")
+            new_c[half] = halves.tile([P, HALF_TILES, H], F32, name="new_c")
+            new_m[half] = halves.tile([P, HALF_TILES, H], F32, name="new_m")
+            hidden[half] = halves.tile([P, HALF_TILES, H], F32, name="hidden")
+            recip[half] = halves.tile([P, HALF_TILES, H], F32, name="recip")
+        act_of, turned_of, mean_var, rstd = {}, {}, {}, {}
+
+        def gates(unit):
+            half, pair = divmod(unit, PAIRS)
+            rows = slice(half * HALF_B, (half + 1) * HALF_B)
+            act = {}
+            for a, gate in enumerate(GATES):
+                sums = gate_psum.tile([P, 2, HALF_B], F32, tag="sums")
+                for jj in range(2):
+                    block = 2 * pair + jj
+                    feats = slice(block * P, (block + 1) * P)
+                    for g in range(PASSES):
+                        nc.tensor.matmul_mx(
+                            out=sums[:, jj, :],
+                            lhsT=w_words[gate][:, g, feats].bitcast(FP8X4),
+                            lhsT_scale=planes[4 * a : P, g, feats],
+                            rhs=codes[:, g, rows].bitcast(FP8X4),
+                            rhs_scale=code_scales[:, g, rows],
+                            start=(g == 0),
+                            stop=(g == PASSES - 1),
+                        )
+                act[gate] = acts.tile([P, 2, HALF_B], F32, name="act_" + gate)
+                for jj in range(2):
+                    block = 2 * pair + jj
+                    nc.scalar.activation(
+                        out=act[gate][:, jj, :],
+                        in_=sums[:, jj, :],
+                        func=gate_func[gate],
+                        bias=bias_cols[:, 8 * a + block : 8 * a + block + 1],
+                        scale=gate_scale[gate],
+                    )
+            act["iz"] = acts.tile([P, 2, HALF_B], F32, name="act_iz")
+            nc.gpsimd.tensor_tensor(out=act["iz"][:], in0=act["i"][:], in1=act["z"][:], op=ALU.mult)
+            act_of[unit] = act
+
+        def turn(unit):
+            turned = {}
+            for name in ("f", "i", "iz", "o"):
+                turned[name] = turn_psum.tile([P, HALF_TILES, PAIR_F], F32, name="turned_" + name, tag="turn")
+                for jj in range(2):
+                    for tt in range(HALF_TILES):
+                        nc.tensor.transpose(
+                            turned[name][:, tt, jj * P : (jj + 1) * P],
+                            act_of[unit][name][:, jj, tt * P : (tt + 1) * P],
+                            ident[:],
+                        )
+            turned_of[unit] = turned
+
+        def update(unit):
+            half, pair = divmod(unit, PAIRS)
+            turned = turned_of[unit]
+            tiles = slice(half * HALF_TILES, (half + 1) * HALF_TILES)
+            feats = slice(pair * PAIR_F, (pair + 1) * PAIR_F)
+            shape = [P, HALF_TILES, PAIR_F]
+            size_iz = work.tile(shape, F32)
+            nc.scalar.activation(out=size_iz[:], in_=turned["iz"][:], func=ACT.Abs)
+            fm2 = work.tile(shape, F32)
+            fc2 = work.tile(shape, F32)
+            fn2 = work.tile(shape, F32)
+            for twice, old in ((fm2, old_m), (fc2, old_c), (fn2, old_n)):
+                nc.vector.scalar_tensor_tensor(
+                    out=twice[:], in0=turned["f"][:], scalar=1.0, in1=old[:, tiles, feats],
+                    op0=ALU.add, op1=ALU.mult,
+                )
+            nc.vector.scalar_tensor_tensor(
+                out=new_m[half][:, :, feats], in0=fm2[:], scalar=0.5, in1=size_iz[:],
+                op0=ALU.mult, op1=ALU.max,
+            )
+            nc.vector.scalar_tensor_tensor(
+                out=new_c[half][:, :, feats], in0=fc2[:], scalar=0.5, in1=turned["iz"][:],
+                op0=ALU.mult, op1=ALU.add,
+            )
+            nc.vector.scalar_tensor_tensor(
+                out=new_n[half][:, :, feats], in0=fn2[:], scalar=0.5, in1=turned["i"][:],
+                op0=ALU.mult, op1=ALU.add,
+            )
+            nc.vector.scalar_tensor_tensor(
+                out=hidden[half][:, :, feats], in0=turned["o"][:], scalar=1.0, in1=new_c[half][:, :, feats],
+                op0=ALU.add, op1=ALU.mult,
+            )
+
+        def store_state(half, part):
+            tiles = slice(half * HALF_TILES, (half + 1) * HALF_TILES)
+            feats = slice(part * 2 * PAIR_F, (part + 1) * 2 * PAIR_F)
+            nc.sync.dma_start(out=by_row_tile(out_3)[:, tiles, feats], in_=new_m[half][:, :, feats])
+            nc.sync.dma_start(out=by_row_tile(out_1)[:, tiles, feats], in_=new_c[half][:, :, feats])
+            nc.sync.dma_start(out=by_row_tile(out_2)[:, tiles, feats], in_=new_n[half][:, :, feats])
+
+        def log_normaliser(half, first_pair, pairs):
+            feats = slice(first_pair * PAIR_F, (first_pair + pairs) * PAIR_F)
+            nc.scalar.activation(
+                out=recip[half][:, :, feats], in_=new_n[half][:, :, feats], func=ACT.Ln, bias=div_eps[:, 0:1]
+            )
+
+        def reciprocal(half, tt):
+            nc.scalar.activation(out=recip[half][:, tt, :], in_=recip[half][:, tt, :], func=ACT.Exp, scale=-1.0)
+
+        def divide(engine, half, tt):
+            row = hidden[half][:, tt, :]
+            engine.tensor_tensor(out=row, in0=row, in1=recip[half][:, tt, :], op=ALU.mult)
+
+        def statistics(half, tt):
+            row = hidden[half][:, tt, :]
+            stats = small.tile([P, H // BN_CHUNK, 6], F32)
+            for c in range(H // BN_CHUNK):
+                nc.vector.bn_stats(out=stats[:, c, :], in_=row[:, c * BN_CHUNK : (c + 1) * BN_CHUNK])
+            mean_var[half, tt] = small.tile([P, 2], F32, name="mean_var")
+            nc.vector.bn_aggr(out=mean_var[half, tt][:], in_=stats[:].rearrange("p c s -> p (c s)"))
+            rstd[half, tt] = small.tile([P, 1], F32, name="rstd")
+            nc.vector.tensor_scalar_add(out=rstd[half, tt][:], in0=mean_var[half, tt][:, 1:2], scalar1=4.0 * LN_EPS)
+            nc.gpsimd.tensor_tensor(out=rstd[half, tt][:], in0=rstd[half, tt][:], in1=minus_half[:], op=ALU.pow)
+
+        def normalise(half):
+            for tt in range(HALF_TILES):
+                row = hidden[half][:, tt, :]
+                nc.vector.scalar_tensor_tensor(
+                    out=row, in0=row, scalar=mean_var[half, tt][:, 0:1], in1=gamma_all[:],
+                    op0=ALU.subtract, op1=ALU.mult,
+                )
+            for tt in range(HALF_TILES):
+                row = hidden[half][:, tt, :]
+                nc.vector.scalar_tensor_tensor(
+                    out=row, in0=row, scalar=rstd[half, tt][:, 0:1], in1=beta_all[:], op0=ALU.mult, op1=ALU.add
+                )
+                nc.sync.dma_start(out=by_row_tile(out_0)[:, half * HALF_TILES + tt, :], in_=row)
+
+        gates(0)
+        for unit in range(UNITS):
+            half, pair = divmod(unit, PAIRS)
+            if PAIRS <= unit + 1 < UNITS:
+                gates(unit + 1)
+            turn(unit)
+            update(unit)
+            if unit + 1 < PAIRS:
+                gates(unit + 1)
+            if pair % 2 == 1:
+                store_state(half, pair // 2)
+            if unit == PAIRS:
+                log_normaliser(0, 0, PAIRS)
+            if unit == PAIRS + 1:
+                reciprocal(0, 0)
+                reciprocal(0, 1)
+                divide(nc.gpsimd, 0, 0)
+            if unit == PAIRS + 2:
+                divide(nc.gpsimd, 0, 1)
+                statistics(0, 0)
+                log_normaliser(1, 0, PAIRS - 1)
+            if unit == PAIRS + 3:
+                statistics(0, 1)
+                normalise(0)
+        log_normaliser(1, PAIRS - 1, 1)
+        reciprocal(1, 0)
+        reciprocal(1, 1)
+        divide(nc.gpsimd, 1, 0)
+        divide(nc.vector, 1, 1)
+        statistics(1, 1)
+        statistics(1, 0)
+        normalise(1)

@@ -26,6 +26,7 @@ HALF_TILES = ROW_TILES // HALVES
 HALF_B = B // HALVES
 PAIR_F = 2 * P
 PAIRS = H // PAIR_F
+PART_F = 2 * PAIR_F
 BN_CHUNK = 512
 
 GATES = ("i", "z", "f", "o")
@@ -75,13 +76,25 @@ def tile_slstmcell_kernel(
         keep = ctx.enter_context(tc.tile_pool(name="keep", bufs=1))
         gate_psum = ctx.enter_context(tc.psum_pool(name="gate_psum", bufs=4))
         turn_psum = ctx.enter_context(tc.psum_pool(name="turn_psum", bufs=4))
+        stage = ctx.enter_context(tc.tile_pool(name="stage", bufs=PASSES))
+        acts = ctx.enter_context(tc.tile_pool(name="acts", bufs=2))
+        work = ctx.enter_context(tc.tile_pool(name="work", bufs=2))
+        halves = ctx.enter_context(tc.tile_pool(name="halves", bufs=HALVES))
+        small = ctx.enter_context(tc.tile_pool(name="small", bufs=ROW_TILES))
 
-        planes = keep.tile([P, PASSES, H], U8, align_bytes=64)
-        nc.vector.memset(planes[:].rearrange("p g n -> p (g n)").bitcast(I32), 0)
+        planes = {}
+        bias_rows = keep.tile([P, P], BF16)
+        for gate in GATES:
+            planes[gate] = keep.tile([P, PASSES, H], U8, name="planes_" + gate, align_bytes=64)
+            nc.vector.memset(planes[gate][:].rearrange("p g n -> p (g n)").bitcast(I32), 0)
+            if gate == GATES[0]:
+                nc.vector.memset(bias_rows[:], 0.0)
         ident = keep.tile([P, P], F32)
         make_identity(nc, ident[:])
         div_eps = keep.tile([P, 1], F32)
+        nc.vector.memset(div_eps[:], DIV_EPS)
         minus_half = keep.tile([P, 1], F32)
+        nc.vector.memset(minus_half[:], -0.5)
 
         w_words = {}
         for gate in GATES:
@@ -94,107 +107,105 @@ def tile_slstmcell_kernel(
         bias_cols = keep.tile([P, 8 * len(GATES)], F32)
         gamma_all = keep.tile([P, H], BF16)
         beta_all = keep.tile([P, H], BF16)
+        x_rows, h_rows = {}, {}
+        for half in range(HALVES):
+            x_rows[half] = keep.tile([P, HALF_TILES, IN], BF16, name="x_rows_%d" % half)
+            h_rows[half] = keep.tile([P, HALF_TILES, H], BF16, name="h_rows_%d" % half)
 
-        def load_weight_columns(pair):
+        def load_combined(half):
+            rows = slice(half * HALF_TILES, (half + 1) * HALF_TILES)
+            nc.sync.dma_start(out=x_rows[half][:], in_=by_row_tile(x)[:, rows, :])
+            nc.sync.dma_start(out=h_rows[half][:], in_=by_row_tile(h_prev)[:, rows, :])
+
+        def load_scales(gate):
+            for r in range(4):
+                nc.sync.dma_start(
+                    out=planes[gate][r : P : 32, :, :].bitcast(I32),
+                    in_=scales_in[gate].rearrange("g (q r) n -> r q g n", r=4)[r].bitcast(I32),
+                )
+
+        def load_weight_columns(pair, some_gates):
             cols = slice(pair * PAIR_F, (pair + 1) * PAIR_F)
-            for gate in GATES:
+            for gate in some_gates:
                 nc.sync.dma_start(
                     out=w_words[gate][:, :, cols].bitcast(I32),
                     in_=words_in[gate].rearrange("g p n t -> p g (n t)").bitcast(I32)[:, :, cols],
                 )
 
-        def load_old_state(half):
+        def load_old_state(half, part):
             rows = slice(half * HALF_TILES, (half + 1) * HALF_TILES)
-            nc.sync.dma_start(out=old_m[:, rows, :], in_=by_row_tile(m_prev)[:, rows, :])
-            nc.sync.dma_start(out=old_c[:, rows, :], in_=by_row_tile(c_prev)[:, rows, :])
-            nc.sync.dma_start(out=old_n[:, rows, :], in_=by_row_tile(n_prev)[:, rows, :])
+            feats = slice(part * PART_F, (part + 1) * PART_F)
+            nc.sync.dma_start(out=old_m[:, rows, feats], in_=by_row_tile(m_prev)[:, rows, feats])
+            nc.sync.dma_start(out=old_c[:, rows, feats], in_=by_row_tile(c_prev)[:, rows, feats])
+            nc.sync.dma_start(out=old_n[:, rows, feats], in_=by_row_tile(n_prev)[:, rows, feats])
 
-        with tc.tile_pool(name="prep", bufs=1) as prep:
-            bias_rows = prep.tile([P, P], BF16)
-            nc.vector.memset(bias_rows[:], 0.0)
-            norm_rows = prep.tile([P, 2, H], BF16)
-            nc.vector.memset(norm_rows[:].rearrange("p v f -> p (v f)").bitcast(I32), 0)
-            ones = prep.tile([P, P], BF16)
-            nc.vector.memset(ones[:], 1.0)
-            nc.vector.memset(div_eps[:], DIV_EPS)
-            nc.vector.memset(minus_half[:], -0.5)
+        load_combined(0)
+        for a, gate in enumerate(GATES):
+            nc.scalar.dma_start(
+                out=bias_rows[8 * a : 8 * a + 8, :],
+                in_=bias_in[gate].rearrange("(j f) -> j f", f=P),
+            )
+        for gate in GATES:
+            load_scales(gate)
+            load_weight_columns(0, (gate,))
+        load_old_state(0, 0)
+        load_weight_columns(1, GATES)
+        load_combined(1)
+        load_weight_columns(2, GATES)
+        load_old_state(0, 1)
+        load_weight_columns(3, GATES)
+        load_old_state(1, 0)
+        load_old_state(1, 1)
+        nc.sync.dma_start(out=gamma_all[:], in_=ln_gamma.partition_broadcast(P))
+        nc.sync.dma_start(out=beta_all[:], in_=ln_beta.partition_broadcast(P))
 
-            combined = prep.tile([P, ROW_TILES, D], BF16)
-            nc.sync.dma_start(out=combined[:, :, 0:IN], in_=by_row_tile(x))
-            nc.sync.dma_start(out=combined[:, :, IN:D], in_=by_row_tile(h_prev))
-            for a, gate in enumerate(GATES):
-                nc.scalar.dma_start(
-                    out=bias_rows[8 * a : 8 * a + 8, :],
-                    in_=bias_in[gate].rearrange("(j f) -> j f", f=P),
+        grouped = {}
+
+        def turn_combined(half, copy_engines):
+            for g in range(PASSES):
+                k_turned = turn_psum.tile([P, 2, HALF_B], F32, tag="turn")
+                for tt in range(HALF_TILES):
+                    if g == 0:
+                        pairs_of_k = x_rows[half][:, tt, :].bitcast(F32)
+                    else:
+                        pairs_of_k = h_rows[half][:, tt, :].bitcast(F32)[:, 256 * (g - 1) : 256 * g]
+                    for u in range(2):
+                        nc.tensor.transpose(
+                            k_turned[:, u, tt * P : (tt + 1) * P],
+                            pairs_of_k[:, u : 256 : 2],
+                            ident[:],
+                        )
+                grouped[half, g] = stage.tile([P, HALF_B, 4], BF16, name="grouped", align_bytes=64)
+                copy_engines[g](
+                    out=grouped[half, g][:].bitcast(F32),
+                    in_=k_turned[:].rearrange("p u b -> p b u"),
                 )
-            nc.scalar.dma_start(out=norm_rows[0:1, 0, :], in_=ln_gamma.rearrange("(o f) -> o f", o=1))
-            nc.scalar.dma_start(out=norm_rows[0:1, 1, :], in_=ln_beta.rearrange("(o f) -> o f", o=1))
-            for a, gate in enumerate(GATES):
-                for r in range(4):
-                    nc.sync.dma_start(
-                        out=planes[4 * a + r : P : 32, :, :].bitcast(I32),
-                        in_=scales_in[gate].rearrange("g (q r) n -> r q g n", r=4)[r].bitcast(I32),
-                    )
-            load_weight_columns(0)
-            load_old_state(0)
-            for pair in range(1, PAIRS):
-                load_weight_columns(pair)
-            load_old_state(1)
 
-            bias_rows_f32 = prep.tile([P, P], F32)
-            nc.vector.tensor_copy(out=bias_rows_f32[:], in_=bias_rows[:])
-            bias_turned = turn_psum.tile([P, P], F32, tag="turn")
-            nc.tensor.transpose(bias_turned[:], bias_rows_f32[:], ident[:])
-            nc.vector.tensor_copy(out=bias_cols[:, 0:16], in_=bias_turned[:, 0:16])
-            nc.vector.tensor_scalar_mul(out=bias_cols[:, 16:32], in0=bias_turned[:, 16:32], scalar1=0.5)
+        def quantise_combined(half):
+            for g in range(PASSES):
+                rows = slice(half * HALF_B, (half + 1) * HALF_B)
+                nc.vector.quantize_mx(
+                    out=codes[:, g, rows].bitcast(FP8X4),
+                    scales=code_scales[:, g, rows],
+                    in_=grouped[half, g][:].rearrange("p b t -> p (b t)"),
+                )
 
-            for half in range(HALVES):
-                grouped = {}
-                for g in range(PASSES):
-                    k_turned = turn_psum.tile([P, 2, HALF_B], F32, tag="turn")
-                    for tt in range(HALF_TILES):
-                        pairs_of_k = combined[:, half * HALF_TILES + tt, :].bitcast(F32)
-                        for u in range(2):
-                            nc.tensor.transpose(
-                                k_turned[:, u, tt * P : (tt + 1) * P],
-                                pairs_of_k[:, 256 * g + u : 256 * (g + 1) : 2],
-                                ident[:],
-                            )
-                    grouped[g] = prep.tile(
-                        [P, HALF_B, 4], BF16, name="grouped_%d_%d" % (half, g), align_bytes=64
-                    )
-                    copy_out = nc.vector.tensor_copy if g % 2 == 0 else nc.scalar.copy
-                    copy_out(
-                        out=grouped[g][:].bitcast(F32),
-                        in_=k_turned[:].rearrange("p u b -> p b u"),
-                    )
-                for g in range(PASSES):
-                    rows = slice(half * HALF_B, (half + 1) * HALF_B)
-                    nc.vector.quantize_mx(
-                        out=codes[:, g, rows].bitcast(FP8X4),
-                        scales=code_scales[:, g, rows],
-                        in_=grouped[g][:].rearrange("p b t -> p (b t)"),
-                    )
+        turn_combined(0, (nc.vector.tensor_copy, nc.scalar.copy, nc.vector.tensor_copy))
+        quantise_combined(0)
 
-            for v, spread in enumerate((gamma_all, beta_all)):
-                for c in range(H // BN_CHUNK):
-                    cols = slice(c * BN_CHUNK, (c + 1) * BN_CHUNK)
-                    summed = gate_psum.tile([P, BN_CHUNK], F32, tag="sums")
-                    nc.tensor.matmul(summed[:], lhsT=ones[:], rhs=norm_rows[:, v, cols], start=True, stop=True)
-                    nc.scalar.copy(out=spread[:, cols], in_=summed[:])
+        bias_rows_f32 = keep.tile([P, P], F32)
+        nc.gpsimd.tensor_copy(out=bias_rows_f32[:], in_=bias_rows[:])
+        bias_turned = turn_psum.tile([P, P], F32, tag="turn")
+        nc.tensor.transpose(bias_turned[:], bias_rows_f32[:], ident[:])
+        nc.scalar.copy(out=bias_cols[:, 0:16], in_=bias_turned[:, 0:16])
+        nc.scalar.mul(out=bias_cols[:, 16:32], in_=bias_turned[:, 16:32], mul=0.5)
 
-        acts = ctx.enter_context(tc.tile_pool(name="acts", bufs=2))
-        work = ctx.enter_context(tc.tile_pool(name="work", bufs=2))
-        halves = ctx.enter_context(tc.tile_pool(name="halves", bufs=HALVES))
-        small = ctx.enter_context(tc.tile_pool(name="small", bufs=ROW_TILES))
-
-        new_n, new_c, new_m, hidden, recip = {}, {}, {}, {}, {}
+        new_n, hidden, recip = {}, {}, {}
         for half in range(HALVES):
             new_n[half] = halves.tile([P, HALF_TILES, H], F32, name="new_n")
-            new_c[half] = halves.tile([P, HALF_TILES, H], F32, name="new_c")
-            new_m[half] = halves.tile([P, HALF_TILES, H], F32, name="new_m")
             hidden[half] = halves.tile([P, HALF_TILES, H], F32, name="hidden")
             recip[half] = halves.tile([P, HALF_TILES, H], F32, name="recip")
+        new_c, new_m = {}, {}
         act_of, turned_of, mean_var, rstd = {}, {}, {}, {}
 
         def gates(unit):
@@ -210,7 +221,7 @@ def tile_slstmcell_kernel(
                         nc.tensor.matmul_mx(
                             out=sums[:, jj, :],
                             lhsT=w_words[gate][:, g, feats].bitcast(FP8X4),
-                            lhsT_scale=planes[4 * a : P, g, feats],
+                            lhsT_scale=planes[gate][:, g, feats],
                             rhs=codes[:, g, rows].bitcast(FP8X4),
                             rhs_scale=code_scales[:, g, rows],
                             start=(g == 0),
@@ -245,10 +256,16 @@ def tile_slstmcell_kernel(
 
         def update(unit):
             half, pair = divmod(unit, PAIRS)
+            part, side = divmod(pair, 2)
             turned = turned_of[unit]
             tiles = slice(half * HALF_TILES, (half + 1) * HALF_TILES)
             feats = slice(pair * PAIR_F, (pair + 1) * PAIR_F)
+            in_part = slice(side * PAIR_F, (side + 1) * PAIR_F)
             shape = [P, HALF_TILES, PAIR_F]
+            if side == 0:
+                new_c[half, part] = work.tile([P, HALF_TILES, PART_F], F32, name="new_c")
+                new_m[half, part] = work.tile([P, HALF_TILES, PART_F], F32, name="new_m")
+            c_here = new_c[half, part][:, :, in_part]
             size_iz = work.tile(shape, F32)
             nc.scalar.activation(out=size_iz[:], in_=turned["iz"][:], func=ACT.Abs)
             fm2 = work.tile(shape, F32)
@@ -260,11 +277,11 @@ def tile_slstmcell_kernel(
                     op0=ALU.add, op1=ALU.mult,
                 )
             nc.vector.scalar_tensor_tensor(
-                out=new_m[half][:, :, feats], in0=fm2[:], scalar=0.5, in1=size_iz[:],
+                out=new_m[half, part][:, :, in_part], in0=fm2[:], scalar=0.5, in1=size_iz[:],
                 op0=ALU.mult, op1=ALU.max,
             )
             nc.vector.scalar_tensor_tensor(
-                out=new_c[half][:, :, feats], in0=fc2[:], scalar=0.5, in1=turned["iz"][:],
+                out=c_here, in0=fc2[:], scalar=0.5, in1=turned["iz"][:],
                 op0=ALU.mult, op1=ALU.add,
             )
             nc.vector.scalar_tensor_tensor(
@@ -272,15 +289,15 @@ def tile_slstmcell_kernel(
                 op0=ALU.mult, op1=ALU.add,
             )
             nc.vector.scalar_tensor_tensor(
-                out=hidden[half][:, :, feats], in0=turned["o"][:], scalar=1.0, in1=new_c[half][:, :, feats],
+                out=hidden[half][:, :, feats], in0=turned["o"][:], scalar=1.0, in1=c_here,
                 op0=ALU.add, op1=ALU.mult,
             )
 
         def store_state(half, part):
             tiles = slice(half * HALF_TILES, (half + 1) * HALF_TILES)
-            feats = slice(part * 2 * PAIR_F, (part + 1) * 2 * PAIR_F)
-            nc.sync.dma_start(out=by_row_tile(out_3)[:, tiles, feats], in_=new_m[half][:, :, feats])
-            nc.sync.dma_start(out=by_row_tile(out_1)[:, tiles, feats], in_=new_c[half][:, :, feats])
+            feats = slice(part * PART_F, (part + 1) * PART_F)
+            nc.sync.dma_start(out=by_row_tile(out_3)[:, tiles, feats], in_=new_m[half, part][:])
+            nc.sync.dma_start(out=by_row_tile(out_1)[:, tiles, feats], in_=new_c[half, part][:])
             nc.sync.dma_start(out=by_row_tile(out_2)[:, tiles, feats], in_=new_n[half][:, :, feats])
 
         def log_normaliser(half, first_pair, pairs):
@@ -321,6 +338,49 @@ def tile_slstmcell_kernel(
                 )
                 nc.sync.dma_start(out=by_row_tile(out_0)[:, half * HALF_TILES + tt, :], in_=row)
 
+        squares = keep.tile([P, H], BF16)
+        minus_mean = {}
+
+        def divide_and_sum(half, tt):
+            row = hidden[half][:, tt, :]
+            total = small.tile([P, 1], F32)
+            nc.vector.scalar_tensor_tensor(
+                out=row, in0=row, scalar=1.0, in1=recip[half][:, tt, :], op0=ALU.mult, op1=ALU.mult,
+                accum_out=total[:],
+            )
+            minus_mean[half, tt] = small.tile([P, 1], F32, name="minus_mean")
+            nc.vector.tensor_scalar_mul(out=minus_mean[half, tt][:], in0=total[:], scalar1=-1.0 / H)
+
+        def squared_deviations(half, tt):
+            sum_sq = small.tile([P, 1], F32)
+            nc.scalar.activation(
+                out=squares[:], in_=hidden[half][:, tt, :], func=ACT.Square,
+                bias=minus_mean[half, tt][:, 0:1], accum_out=sum_sq[:],
+            )
+            rstd[half, tt] = small.tile([P, 1], F32, name="rstd")
+            nc.gpsimd.tensor_scalar(
+                out=rstd[half, tt][:], in0=sum_sq[:], scalar1=1.0 / H, scalar2=4.0 * LN_EPS,
+                op0=ALU.mult, op1=ALU.add,
+            )
+            nc.gpsimd.tensor_tensor(out=rstd[half, tt][:], in0=rstd[half, tt][:], in1=minus_half[:], op=ALU.pow)
+
+        def centre(half, tt):
+            nc.vector.scalar_tensor_tensor(
+                out=recip[half][:, tt, :], in0=hidden[half][:, tt, :], scalar=minus_mean[half, tt][:, 0:1],
+                in1=gamma_all[:], op0=ALU.add, op1=ALU.mult,
+            )
+
+        def scale_and_store(half, tt):
+            for c in range(H // BN_CHUNK):
+                cols = slice(c * BN_CHUNK, (c + 1) * BN_CHUNK)
+                nc.vector.scalar_tensor_tensor(
+                    out=recip[half][:, tt, cols], in0=recip[half][:, tt, cols], scalar=rstd[half, tt][:, 0:1],
+                    in1=beta_all[:, cols], op0=ALU.mult, op1=ALU.add,
+                )
+                nc.sync.dma_start(
+                    out=by_row_tile(out_0)[:, half * HALF_TILES + tt, cols], in_=recip[half][:, tt, cols]
+                )
+
         gates(0)
         for unit in range(UNITS):
             half, pair = divmod(unit, PAIRS)
@@ -328,6 +388,9 @@ def tile_slstmcell_kernel(
                 gates(unit + 1)
             turn(unit)
             update(unit)
+            if unit == 1:
+                turn_combined(1, (nc.scalar.copy, nc.scalar.copy, nc.scalar.copy))
+                quantise_combined(1)
             if unit + 1 < PAIRS:
                 gates(unit + 1)
             if pair % 2 == 1:
@@ -346,10 +409,13 @@ def tile_slstmcell_kernel(
                 statistics(0, 1)
                 normalise(0)
         log_normaliser(1, PAIRS - 1, 1)
-        reciprocal(1, 0)
-        reciprocal(1, 1)
-        divide(nc.gpsimd, 1, 0)
-        divide(nc.vector, 1, 1)
-        statistics(1, 1)
-        statistics(1, 0)
-        normalise(1)
+        for tt in range(HALF_TILES):
+            reciprocal(1, tt)
+        for tt in range(HALF_TILES):
+            divide_and_sum(1, tt)
+        for tt in range(HALF_TILES):
+            squared_deviations(1, tt)
+        for tt in range(HALF_TILES):
+            centre(1, tt)
+        for tt in range(HALF_TILES):
+            scale_and_store(1, tt)

@@ -145,12 +145,12 @@ def tile_slstmcell_kernel(
                 out=bias_rows[8 * a : 8 * a + 8, :],
                 in_=bias_in[gate].rearrange("(j f) -> j f", f=P),
             )
+        load_combined(1)
         for gate in GATES:
             load_scales(gate)
             load_weight_columns(0, (gate,))
         load_old_state(0, 0)
         load_weight_columns(1, GATES)
-        load_combined(1)
         load_weight_columns(2, GATES)
         load_old_state(0, 1)
         load_weight_columns(3, GATES)
@@ -199,6 +199,8 @@ def tile_slstmcell_kernel(
         nc.tensor.transpose(bias_turned[:], bias_rows_f32[:], ident[:])
         nc.scalar.copy(out=bias_cols[:, 0:16], in_=bias_turned[:, 0:16])
         nc.scalar.mul(out=bias_cols[:, 16:32], in_=bias_turned[:, 16:32], mul=0.5)
+        turn_combined(1, (nc.scalar.copy, nc.scalar.copy, nc.scalar.copy))
+        quantise_combined(1)
 
         new_n, hidden, recip = {}, {}, {}
         for half in range(HALVES):
@@ -208,12 +210,14 @@ def tile_slstmcell_kernel(
         new_c, new_m = {}, {}
         act_of, turned_of, mean_var, rstd = {}, {}, {}, {}
 
-        def gates(unit):
+        sums_of = {}
+
+        def mx(unit, some_gates=GATES):
             half, pair = divmod(unit, PAIRS)
             rows = slice(half * HALF_B, (half + 1) * HALF_B)
-            act = {}
-            for a, gate in enumerate(GATES):
+            for gate in some_gates:
                 sums = gate_psum.tile([P, 2, HALF_B], F32, tag="sums")
+                sums_of[unit, gate] = sums
                 for jj in range(2):
                     block = 2 * pair + jj
                     feats = slice(block * P, (block + 1) * P)
@@ -227,6 +231,13 @@ def tile_slstmcell_kernel(
                             start=(g == 0),
                             stop=(g == PASSES - 1),
                         )
+
+        def act_(unit, some_gates=GATES):
+            half, pair = divmod(unit, PAIRS)
+            act = act_of.setdefault(unit, {})
+            for gate in some_gates:
+                a = GATES.index(gate)
+                sums = sums_of[unit, gate]
                 act[gate] = acts.tile([P, 2, HALF_B], F32, name="act_" + gate)
                 for jj in range(2):
                     block = 2 * pair + jj
@@ -237,13 +248,23 @@ def tile_slstmcell_kernel(
                         bias=bias_cols[:, 8 * a + block : 8 * a + block + 1],
                         scale=gate_scale[gate],
                     )
-            act["iz"] = acts.tile([P, 2, HALF_B], F32, name="act_iz")
-            nc.gpsimd.tensor_tensor(out=act["iz"][:], in0=act["i"][:], in1=act["z"][:], op=ALU.mult)
-            act_of[unit] = act
+                if gate == "z":
+                    act["iz"] = acts.tile([P, 2, HALF_B], F32, name="act_iz")
+                    nc.gpsimd.tensor_tensor(out=act["iz"][:], in0=act["i"][:], in1=act["z"][:], op=ALU.mult)
 
-        def turn(unit):
-            turned = {}
-            for name in ("f", "i", "iz", "o"):
+        def gates(unit):
+            for gate in GATES:
+                mx(unit, (gate,))
+                act_(unit, (gate,))
+
+        def gates_rest(unit):
+            for gate in GATES[1:]:
+                mx(unit, (gate,))
+                act_(unit, (gate,))
+
+        def turn(unit, names=("f", "i", "iz", "o")):
+            turned = turned_of.setdefault(unit, {})
+            for name in names:
                 turned[name] = turn_psum.tile([P, HALF_TILES, PAIR_F], F32, name="turned_" + name, tag="turn")
                 for jj in range(2):
                     for tt in range(HALF_TILES):
@@ -252,9 +273,20 @@ def tile_slstmcell_kernel(
                             act_of[unit][name][:, jj, tt * P : (tt + 1) * P],
                             ident[:],
                         )
-            turned_of[unit] = turned
 
-        def update(unit):
+        size_of = {}
+
+        def absz(unit):
+            size_of[unit] = work.tile([P, HALF_TILES, PAIR_F], F32, name="size_iz")
+            nc.scalar.activation(out=size_of[unit][:], in_=turned_of[unit]["iz"][:], func=ACT.Abs)
+
+        N_FIRST = ("fn2", "fc2", "n", "fm2", "m", "c", "oc")
+
+        def update(unit, order=("fm2", "fc2", "fn2", "m", "c", "n", "oc")):
+            absz(unit)
+            upd(unit, order)
+
+        def upd(unit, order=("fm2", "fc2", "fn2", "m", "c", "n", "oc")):
             half, pair = divmod(unit, PAIRS)
             part, side = divmod(pair, 2)
             turned = turned_of[unit]
@@ -266,32 +298,38 @@ def tile_slstmcell_kernel(
                 new_c[half, part] = work.tile([P, HALF_TILES, PART_F], F32, name="new_c")
                 new_m[half, part] = work.tile([P, HALF_TILES, PART_F], F32, name="new_m")
             c_here = new_c[half, part][:, :, in_part]
-            size_iz = work.tile(shape, F32)
-            nc.scalar.activation(out=size_iz[:], in_=turned["iz"][:], func=ACT.Abs)
+            size_iz = size_of[unit]
             fm2 = work.tile(shape, F32)
             fc2 = work.tile(shape, F32)
             fn2 = work.tile(shape, F32)
-            for twice, old in ((fm2, old_m), (fc2, old_c), (fn2, old_n)):
-                nc.vector.scalar_tensor_tensor(
-                    out=twice[:], in0=turned["f"][:], scalar=1.0, in1=old[:, tiles, feats],
-                    op0=ALU.add, op1=ALU.mult,
-                )
-            nc.vector.scalar_tensor_tensor(
-                out=new_m[half, part][:, :, in_part], in0=fm2[:], scalar=0.5, in1=size_iz[:],
-                op0=ALU.mult, op1=ALU.max,
-            )
-            nc.vector.scalar_tensor_tensor(
-                out=c_here, in0=fc2[:], scalar=0.5, in1=turned["iz"][:],
-                op0=ALU.mult, op1=ALU.add,
-            )
-            nc.vector.scalar_tensor_tensor(
-                out=new_n[half][:, :, feats], in0=fn2[:], scalar=0.5, in1=turned["i"][:],
-                op0=ALU.mult, op1=ALU.add,
-            )
-            nc.vector.scalar_tensor_tensor(
-                out=hidden[half][:, :, feats], in0=turned["o"][:], scalar=1.0, in1=c_here,
-                op0=ALU.add, op1=ALU.mult,
-            )
+            twice_of = {"fm2": (fm2, old_m), "fc2": (fc2, old_c), "fn2": (fn2, old_n)}
+            for step in order:
+                if step in twice_of:
+                    twice, old = twice_of[step]
+                    nc.vector.scalar_tensor_tensor(
+                        out=twice[:], in0=turned["f"][:], scalar=1.0, in1=old[:, tiles, feats],
+                        op0=ALU.add, op1=ALU.mult,
+                    )
+                if step == "m":
+                    nc.vector.scalar_tensor_tensor(
+                        out=new_m[half, part][:, :, in_part], in0=fm2[:], scalar=0.5, in1=size_iz[:],
+                        op0=ALU.mult, op1=ALU.max,
+                    )
+                if step == "c":
+                    nc.vector.scalar_tensor_tensor(
+                        out=c_here, in0=fc2[:], scalar=0.5, in1=turned["iz"][:],
+                        op0=ALU.mult, op1=ALU.add,
+                    )
+                if step == "n":
+                    nc.vector.scalar_tensor_tensor(
+                        out=new_n[half][:, :, feats], in0=fn2[:], scalar=0.5, in1=turned["i"][:],
+                        op0=ALU.mult, op1=ALU.add,
+                    )
+                if step == "oc":
+                    nc.vector.scalar_tensor_tensor(
+                        out=hidden[half][:, :, feats], in0=turned["o"][:], scalar=1.0, in1=c_here,
+                        op0=ALU.add, op1=ALU.mult,
+                    )
 
         def store_state(half, part):
             tiles = slice(half * HALF_TILES, (half + 1) * HALF_TILES)
@@ -303,11 +341,18 @@ def tile_slstmcell_kernel(
         def log_normaliser(half, first_pair, pairs):
             feats = slice(first_pair * PAIR_F, (first_pair + pairs) * PAIR_F)
             nc.scalar.activation(
-                out=recip[half][:, :, feats], in_=new_n[half][:, :, feats], func=ACT.Ln, bias=div_eps[:, 0:1]
+                out=recip[half][:, :, feats], in_=new_n[half][:, :, feats], func=ACT.Square, bias=div_eps[:, 0:1]
             )
 
+        def ars(half, first_pair, pairs):
+            feats = slice(first_pair * PAIR_F, (first_pair + pairs) * PAIR_F)
+            nc.scalar.activation(out=recip[half][:, :, feats], in_=recip[half][:, :, feats], func=ACT.Abs_reciprocal_sqrt)
+
+        def rstd_of(half, tt):
+            nc.gpsimd.tensor_tensor(out=rstd[half, tt][:], in0=rstd[half, tt][:], in1=minus_half[:], op=ALU.pow)
+
         def reciprocal(half, tt):
-            nc.scalar.activation(out=recip[half][:, tt, :], in_=recip[half][:, tt, :], func=ACT.Exp, scale=-1.0)
+            nc.scalar.activation(out=recip[half][:, tt, :], in_=recip[half][:, tt, :], func=ACT.Abs_reciprocal_sqrt)
 
         def divide(engine, half, tt):
             row = hidden[half][:, tt, :]
@@ -322,7 +367,6 @@ def tile_slstmcell_kernel(
             nc.vector.bn_aggr(out=mean_var[half, tt][:], in_=stats[:].rearrange("p c s -> p (c s)"))
             rstd[half, tt] = small.tile([P, 1], F32, name="rstd")
             nc.vector.tensor_scalar_add(out=rstd[half, tt][:], in0=mean_var[half, tt][:, 1:2], scalar1=4.0 * LN_EPS)
-            nc.gpsimd.tensor_tensor(out=rstd[half, tt][:], in0=rstd[half, tt][:], in1=minus_half[:], op=ALU.pow)
 
         def normalise(half):
             for tt in range(HALF_TILES):
@@ -382,35 +426,46 @@ def tile_slstmcell_kernel(
                 )
 
         gates(0)
-        for unit in range(UNITS):
-            half, pair = divmod(unit, PAIRS)
-            if PAIRS <= unit + 1 < UNITS:
-                gates(unit + 1)
+        for unit in range(PAIRS):
+            if unit > 0:
+                mx(unit + 1, ("i",)); act_(unit + 1, ("i",))
             turn(unit)
-            update(unit)
-            if unit == 1:
-                turn_combined(1, (nc.scalar.copy, nc.scalar.copy, nc.scalar.copy))
-                quantise_combined(1)
-            if unit + 1 < PAIRS:
-                gates(unit + 1)
-            if pair % 2 == 1:
-                store_state(half, pair // 2)
-            if unit == PAIRS:
-                log_normaliser(0, 0, PAIRS)
-            if unit == PAIRS + 1:
-                reciprocal(0, 0)
-                reciprocal(0, 1)
-                divide(nc.gpsimd, 0, 0)
-            if unit == PAIRS + 2:
-                divide(nc.gpsimd, 0, 1)
-                statistics(0, 0)
-                log_normaliser(1, 0, PAIRS - 1)
-            if unit == PAIRS + 3:
-                statistics(0, 1)
-                normalise(0)
-        log_normaliser(1, PAIRS - 1, 1)
-        for tt in range(HALF_TILES):
-            reciprocal(1, tt)
+            if unit == PAIRS - 1:
+                update(unit, N_FIRST)
+            else:
+                update(unit)
+            if unit > 0:
+                log_normaliser(0, unit - 1, 1)
+            if unit % 2 == 1:
+                store_state(0, unit // 2)
+            if unit == 0:
+                mx(unit + 1, ("i",)); act_(unit + 1, ("i",))
+            gates_rest(unit + 1)
+        log_normaliser(0, 3, 1)
+        mx(5, ("i",))
+        turn(4)
+        absz(4)
+        reciprocal(0, 0); reciprocal(0, 1)
+        upd(4, ("fm2", "fc2", "fn2", "n", "m", "c", "oc"))
+        act_(5, ("i",))
+        divide(nc.vector, 0, 0); divide(nc.vector, 0, 1)
+        statistics(0, 0); statistics(0, 1)
+        gates_rest(5); rstd_of(0, 0); rstd_of(0, 1)
+        mx(6, ("i",)); act_(6, ("i",))
+        turn(5); update(5); store_state(1, 0)
+        log_normaliser(1, 0, 1)
+        normalise(0)
+        gates_rest(6)
+        mx(7, ("i",)); act_(7, ("i",))
+        turn(6); update(6)
+        log_normaliser(1, 1, 1)
+        gates_rest(7)
+        ars(1, 0, 2)
+        log_normaliser(1, 2, 1)
+        ars(1, 2, 1)
+        turn(7); update(7, N_FIRST); store_state(1, 1)
+        log_normaliser(1, 3, 1)
+        ars(1, 3, 1)
         for tt in range(HALF_TILES):
             divide_and_sum(1, tt)
         for tt in range(HALF_TILES):

@@ -280,7 +280,7 @@ def tile_slstmcell_kernel(
             size_of[unit] = work.tile([P, HALF_TILES, PAIR_F], F32, name="size_iz")
             nc.scalar.activation(out=size_of[unit][:], in_=turned_of[unit]["iz"][:], func=ACT.Abs)
 
-        N_FIRST = ("fn2", "fc2", "n", "fm2", "m", "c", "oc")
+        N_FIRST = ("fn2", "fc2", "fm2", "n", "c", "m", "oc")
 
         def update(unit, order=("fm2", "fc2", "fn2", "m", "c", "n", "oc")):
             absz(unit)
@@ -358,15 +358,19 @@ def tile_slstmcell_kernel(
             row = hidden[half][:, tt, :]
             engine.tensor_tensor(out=row, in0=row, in1=recip[half][:, tt, :], op=ALU.mult)
 
-        def statistics(half, tt):
-            row = hidden[half][:, tt, :]
-            stats = small.tile([P, H // BN_CHUNK, 6], F32)
-            for c in range(H // BN_CHUNK):
-                nc.vector.bn_stats(out=stats[:, c, :], in_=row[:, c * BN_CHUNK : (c + 1) * BN_CHUNK])
-            mean_var[half, tt] = small.tile([P, 2], F32, name="mean_var")
-            nc.vector.bn_aggr(out=mean_var[half, tt][:], in_=stats[:].rearrange("p c s -> p (c s)"))
-            rstd[half, tt] = small.tile([P, 1], F32, name="rstd")
-            nc.vector.tensor_scalar_add(out=rstd[half, tt][:], in0=mean_var[half, tt][:, 1:2], scalar1=4.0 * LN_EPS)
+        def statistics(half):
+            stats = {}
+            for tt in range(HALF_TILES):
+                row = hidden[half][:, tt, :]
+                stats[tt] = small.tile([P, H // BN_CHUNK, 6], F32, name="stats")
+                for c in range(H // BN_CHUNK):
+                    nc.vector.bn_stats(out=stats[tt][:, c, :], in_=row[:, c * BN_CHUNK : (c + 1) * BN_CHUNK])
+            for tt in range(HALF_TILES):
+                mean_var[half, tt] = small.tile([P, 2], F32, name="mean_var")
+                nc.vector.bn_aggr(out=mean_var[half, tt][:], in_=stats[tt][:].rearrange("p c s -> p (c s)"))
+            for tt in range(HALF_TILES):
+                rstd[half, tt] = small.tile([P, 1], F32, name="rstd")
+                nc.vector.tensor_scalar_add(out=rstd[half, tt][:], in0=mean_var[half, tt][:, 1:2], scalar1=4.0 * LN_EPS)
 
         def normalise(half):
             for tt in range(HALF_TILES):
@@ -383,30 +387,35 @@ def tile_slstmcell_kernel(
                 nc.sync.dma_start(out=by_row_tile(out_0)[:, half * HALF_TILES + tt, :], in_=row)
 
         squares = keep.tile([P, H], BF16)
-        minus_mean = {}
+        minus_mean, total, sum_sq = {}, {}, {}
+        ln_eps4 = keep.tile([P, 1], F32)
+        nc.vector.memset(ln_eps4[:], 4.0 * LN_EPS)
 
         def divide_and_sum(half, tt):
             row = hidden[half][:, tt, :]
-            total = small.tile([P, 1], F32)
+            total[half, tt] = small.tile([P, 1], F32, name="total")
             nc.vector.scalar_tensor_tensor(
                 out=row, in0=row, scalar=1.0, in1=recip[half][:, tt, :], op0=ALU.mult, op1=ALU.mult,
-                accum_out=total[:],
+                accum_out=total[half, tt][:],
             )
+
+        def negative_mean(half, tt):
             minus_mean[half, tt] = small.tile([P, 1], F32, name="minus_mean")
-            nc.vector.tensor_scalar_mul(out=minus_mean[half, tt][:], in0=total[:], scalar1=-1.0 / H)
+            nc.scalar.mul(out=minus_mean[half, tt][:], in_=total[half, tt][:], mul=-1.0 / H)
 
         def squared_deviations(half, tt):
-            sum_sq = small.tile([P, 1], F32)
+            sum_sq[half, tt] = small.tile([P, 1], F32, name="sum_sq")
             nc.scalar.activation(
                 out=squares[:], in_=hidden[half][:, tt, :], func=ACT.Square,
-                bias=minus_mean[half, tt][:, 0:1], accum_out=sum_sq[:],
+                bias=minus_mean[half, tt][:, 0:1], accum_out=sum_sq[half, tt][:],
             )
+
+        def inverse_deviation(half, tt):
             rstd[half, tt] = small.tile([P, 1], F32, name="rstd")
-            nc.gpsimd.tensor_scalar(
-                out=rstd[half, tt][:], in0=sum_sq[:], scalar1=1.0 / H, scalar2=4.0 * LN_EPS,
-                op0=ALU.mult, op1=ALU.add,
+            nc.scalar.activation(
+                out=rstd[half, tt][:], in_=sum_sq[half, tt][:], func=ACT.Abs_reciprocal_sqrt, scale=1.0 / H,
+                bias=ln_eps4[:, 0:1],
             )
-            nc.gpsimd.tensor_tensor(out=rstd[half, tt][:], in0=rstd[half, tt][:], in1=minus_half[:], op=ALU.pow)
 
         def centre(half, tt):
             nc.vector.scalar_tensor_tensor(
@@ -446,10 +455,10 @@ def tile_slstmcell_kernel(
         turn(4)
         absz(4)
         reciprocal(0, 0); reciprocal(0, 1)
-        upd(4, ("fm2", "fc2", "fn2", "n", "m", "c", "oc"))
+        upd(4, N_FIRST)
         act_(5, ("i",))
         divide(nc.vector, 0, 0); divide(nc.vector, 0, 1)
-        statistics(0, 0); statistics(0, 1)
+        statistics(0)
         gates_rest(5); rstd_of(0, 0); rstd_of(0, 1)
         mx(6, ("i",)); act_(6, ("i",))
         turn(5); update(5); store_state(1, 0)
@@ -468,8 +477,12 @@ def tile_slstmcell_kernel(
         ars(1, 3, 1)
         for tt in range(HALF_TILES):
             divide_and_sum(1, tt)
-        for tt in range(HALF_TILES):
-            squared_deviations(1, tt)
+        negative_mean(1, 0)
+        squared_deviations(1, 0)
+        negative_mean(1, 1)
+        inverse_deviation(1, 0)
+        squared_deviations(1, 1)
+        inverse_deviation(1, 1)
         for tt in range(HALF_TILES):
             centre(1, tt)
         for tt in range(HALF_TILES):

@@ -417,6 +417,10 @@ def tile_slstmcell_kernel(
                 bias=ln_eps4[:, 0:1],
             )
 
+        def preload_reciprocal_table():
+            scratch = small.tile([P, 1], F32)
+            nc.scalar.activation(out=scratch[:], in_=ln_eps4[:], func=ACT.Abs_reciprocal_sqrt)
+
         def centre(half, tt):
             nc.vector.scalar_tensor_tensor(
                 out=recip[half][:, tt, :], in0=hidden[half][:, tt, :], scalar=minus_mean[half, tt][:, 0:1],
@@ -435,55 +439,44 @@ def tile_slstmcell_kernel(
                 )
 
         gates(0)
-        for unit in range(PAIRS):
-            if unit > 0:
+        for unit in range(UNITS):
+            half, pair = divmod(unit, PAIRS)
+            if 0 < unit < UNITS - 1:
                 mx(unit + 1, ("i",)); act_(unit + 1, ("i",))
             turn(unit)
-            if unit == PAIRS - 1:
-                update(unit, N_FIRST)
+            if unit == UNITS - 1:
+                preload_reciprocal_table()
+                absz(unit)
+                reciprocal(0, 0); reciprocal(0, 1)
+                upd(unit, N_FIRST)
             else:
                 update(unit)
             if unit > 0:
-                log_normaliser(0, unit - 1, 1)
-            if unit % 2 == 1:
-                store_state(0, unit // 2)
+                log_normaliser((unit - 1) // PAIRS, (unit - 1) % PAIRS, 1)
+            if pair % 2 == 1:
+                store_state(half, pair // 2)
             if unit == 0:
                 mx(unit + 1, ("i",)); act_(unit + 1, ("i",))
-            gates_rest(unit + 1)
-        log_normaliser(0, 3, 1)
-        mx(5, ("i",))
-        turn(4)
-        absz(4)
-        reciprocal(0, 0); reciprocal(0, 1)
-        upd(4, N_FIRST)
-        act_(5, ("i",))
-        divide(nc.vector, 0, 0); divide(nc.vector, 0, 1)
-        statistics(0)
-        gates_rest(5); rstd_of(0, 0); rstd_of(0, 1)
-        mx(6, ("i",)); act_(6, ("i",))
-        turn(5); update(5); store_state(1, 0)
-        log_normaliser(1, 0, 1)
-        normalise(0)
-        gates_rest(6)
-        mx(7, ("i",)); act_(7, ("i",))
-        turn(6); update(6)
-        log_normaliser(1, 1, 1)
-        gates_rest(7)
-        ars(1, 0, 2)
-        log_normaliser(1, 2, 1)
-        ars(1, 2, 1)
-        turn(7); update(7, N_FIRST); store_state(1, 1)
+            if unit < UNITS - 1:
+                gates_rest(unit + 1)
+        ars(1, 0, 3)
+        divide_and_sum(0, 0); divide_and_sum(0, 1)
+        negative_mean(0, 0)
+        squared_deviations(0, 0)
+        negative_mean(0, 1)
+        inverse_deviation(0, 0)
+        squared_deviations(0, 1)
+        inverse_deviation(0, 1)
+        centre(0, 0); centre(0, 1)
         log_normaliser(1, 3, 1)
         ars(1, 3, 1)
-        for tt in range(HALF_TILES):
-            divide_and_sum(1, tt)
+        scale_and_store(0, 0); scale_and_store(0, 1)
+        divide_and_sum(1, 0); divide_and_sum(1, 1)
         negative_mean(1, 0)
         squared_deviations(1, 0)
         negative_mean(1, 1)
         inverse_deviation(1, 0)
         squared_deviations(1, 1)
         inverse_deviation(1, 1)
-        for tt in range(HALF_TILES):
-            centre(1, tt)
-        for tt in range(HALF_TILES):
-            scale_and_store(1, tt)
+        centre(1, 0); centre(1, 1)
+        scale_and_store(1, 0); scale_and_store(1, 1)

@@ -201,6 +201,17 @@ def tile_slstmcell_kernel(
         nc.scalar.mul(out=bias_cols[:, 16:32], in_=bias_turned[:, 16:32], mul=0.5)
         turn_combined(1, (nc.scalar.copy, nc.scalar.copy, nc.scalar.copy))
         quantise_combined(1)
+        half_bo = keep.tile([P, HALF_TILES, H], BF16)
+        for c in range(H // BN_CHUNK):
+            spread = turn_psum.tile([P, BN_CHUNK], F32, tag="turn")
+            for j in range(BN_CHUNK // P):
+                col = 8 * GATES.index("o") + c * (BN_CHUNK // P) + j
+                nc.tensor.matmul(
+                    spread[:, j * P : (j + 1) * P], lhsT=bias_cols[:, col : col + 1].to_broadcast([P, P]),
+                    rhs=ident[:], start=True, stop=True,
+                )
+            for tt in range(HALF_TILES):
+                nc.scalar.copy(out=half_bo[:, tt, c * BN_CHUNK : (c + 1) * BN_CHUNK], in_=spread[:])
 
         new_n, hidden, recip = {}, {}, {}
         for half in range(HALVES):
@@ -218,6 +229,21 @@ def tile_slstmcell_kernel(
             for gate in some_gates:
                 sums = gate_psum.tile([P, 2, HALF_B], F32, tag="sums")
                 sums_of[unit, gate] = sums
+                if gate == "o":
+                    feats = slice(pair * PAIR_F, (pair + 1) * PAIR_F)
+                    for tt in range(HALF_TILES):
+                        tile_rows = slice((half * HALF_TILES + tt) * P, (half * HALF_TILES + tt + 1) * P)
+                        for g in range(PASSES):
+                            nc.tensor.matmul_mx(
+                                out=sums[:, tt, :],
+                                lhsT=codes[:, g, tile_rows].bitcast(FP8X4),
+                                lhsT_scale=code_scales[:, g, tile_rows],
+                                rhs=w_words[gate][:, g, feats].bitcast(FP8X4),
+                                rhs_scale=planes[gate][:, g, feats],
+                                start=(g == 0),
+                                stop=(g == PASSES - 1),
+                            )
+                    continue
                 for jj in range(2):
                     block = 2 * pair + jj
                     feats = slice(block * P, (block + 1) * P)
@@ -252,6 +278,22 @@ def tile_slstmcell_kernel(
                     act["iz"] = acts.tile([P, 2, HALF_B], F32, name="act_iz")
                     nc.gpsimd.tensor_tensor(out=act["iz"][:], in0=act["i"][:], in1=act["z"][:], op=ALU.mult)
 
+        halved_of = {}
+
+        def add_o(unit):
+            half, pair = divmod(unit, PAIRS)
+            feats = slice(pair * PAIR_F, (pair + 1) * PAIR_F)
+            halved_of[unit] = work.tile([P, HALF_TILES, PAIR_F], F32, name="halved")
+            nc.vector.scalar_tensor_tensor(
+                out=halved_of[unit][:], in0=sums_of[unit, "o"][:], scalar=0.5, in1=half_bo[:, :, feats],
+                op0=ALU.mult, op1=ALU.add,
+            )
+
+        def tanh_o(unit):
+            act = act_of.setdefault(unit, {})
+            act["o"] = acts.tile([P, 2, HALF_B], F32, name="act_o")
+            nc.scalar.activation(out=act["o"][:], in_=halved_of[unit][:], func=ACT.Tanh)
+
         def gates(unit):
             for gate in GATES:
                 mx(unit, (gate,))
@@ -262,7 +304,7 @@ def tile_slstmcell_kernel(
                 mx(unit, (gate,))
                 act_(unit, (gate,))
 
-        def turn(unit, names=("f", "i", "iz", "o")):
+        def turn(unit, names=("f", "i", "iz")):
             turned = turned_of.setdefault(unit, {})
             for name in names:
                 turned[name] = turn_psum.tile([P, HALF_TILES, PAIR_F], F32, name="turned_" + name, tag="turn")
@@ -294,14 +336,17 @@ def tile_slstmcell_kernel(
             feats = slice(pair * PAIR_F, (pair + 1) * PAIR_F)
             in_part = slice(side * PAIR_F, (side + 1) * PAIR_F)
             shape = [P, HALF_TILES, PAIR_F]
-            if side == 0:
+            if side == 0 and order[0] != "oc":
                 new_c[half, part] = work.tile([P, HALF_TILES, PART_F], F32, name="new_c")
                 new_m[half, part] = work.tile([P, HALF_TILES, PART_F], F32, name="new_m")
             c_here = new_c[half, part][:, :, in_part]
             size_iz = size_of[unit]
-            fm2 = work.tile(shape, F32)
-            fc2 = work.tile(shape, F32)
-            fn2 = work.tile(shape, F32)
+            if order[0] != "oc":
+                fm2 = work.tile(shape, F32)
+                fc2 = work.tile(shape, F32)
+                fn2 = work.tile(shape, F32)
+            else:
+                fm2 = fc2 = fn2 = None
             twice_of = {"fm2": (fm2, old_m), "fc2": (fc2, old_c), "fn2": (fn2, old_n)}
             for step in order:
                 if step in twice_of:
@@ -327,9 +372,12 @@ def tile_slstmcell_kernel(
                     )
                 if step == "oc":
                     nc.vector.scalar_tensor_tensor(
-                        out=hidden[half][:, :, feats], in0=turned["o"][:], scalar=1.0, in1=c_here,
+                        out=hidden[half][:, :, feats], in0=act_of[unit]["o"][:], scalar=1.0, in1=c_here,
                         op0=ALU.add, op1=ALU.mult,
                     )
+
+        def upd_oc(unit):
+            upd(unit, ("oc",))
 
         def store_state(half, part):
             tiles = slice(half * HALF_TILES, (half + 1) * HALF_TILES)
@@ -438,27 +486,38 @@ def tile_slstmcell_kernel(
                     out=by_row_tile(out_0)[:, half * HALF_TILES + tt, cols], in_=recip[half][:, tt, cols]
                 )
 
-        gates(0)
+        for gate in ("i", "z", "f"):
+            mx(0, (gate,)); act_(0, (gate,))
+        mx(0, ("o",)); add_o(0); tanh_o(0)
+        started = set()
         for unit in range(UNITS):
             half, pair = divmod(unit, PAIRS)
-            if 0 < unit < UNITS - 1:
-                mx(unit + 1, ("i",)); act_(unit + 1, ("i",))
+            last = unit == UNITS - 1
             turn(unit)
-            if unit == UNITS - 1:
+            if last:
                 preload_reciprocal_table()
-                absz(unit)
+            absz(unit)
+            if last:
                 reciprocal(0, 0); reciprocal(0, 1)
-                upd(unit, N_FIRST)
+            if not last:
+                for gate in ("i", "z", "f"):
+                    if (unit + 1, gate) not in started:
+                        mx(unit + 1, (gate,)); act_(unit + 1, (gate,))
+                mx(unit + 1, ("o",))
+            if last:
+                upd(unit, ("fn2", "fc2", "fm2", "n", "c", "m"))
             else:
-                update(unit)
+                upd(unit, ("fm2", "fc2", "fn2", "m", "c", "n"))
+                add_o(unit + 1)
+            upd_oc(unit)
             if unit > 0:
                 log_normaliser((unit - 1) // PAIRS, (unit - 1) % PAIRS, 1)
+            if unit + 2 < UNITS:
+                mx(unit + 2, ("i",)); act_(unit + 2, ("i",)); started.add((unit + 2, "i"))
+            if not last:
+                tanh_o(unit + 1)
             if pair % 2 == 1:
                 store_state(half, pair // 2)
-            if unit == 0:
-                mx(unit + 1, ("i",)); act_(unit + 1, ("i",))
-            if unit < UNITS - 1:
-                gates_rest(unit + 1)
         ars(1, 0, 3)
         divide_and_sum(0, 0); divide_and_sum(0, 1)
         negative_mean(0, 0)

@@ -26,11 +26,13 @@ HALF_TILES = ROW_TILES // HALVES
 HALF_B = B // HALVES
 PAIR_F = 2 * P
 PAIRS = H // PAIR_F
+UNITS = HALVES * PAIRS
 PART_F = 2 * PAIR_F
-BN_CHUNK = 512
+BANK = 512
+BLOCKS = H // P
 
 GATES = ("i", "z", "f", "o")
-UNITS = HALVES * PAIRS
+TURNED = ("f", "i", "iz")
 
 FLOPS = 2 * B * D * 4 * H
 
@@ -65,8 +67,8 @@ def tile_slstmcell_kernel(
     words_in = {"i": Wi_words, "z": Wz_words, "f": Wf_words, "o": Wo_words}
     scales_in = {"i": Wi_scales, "z": Wz_scales, "f": Wf_scales, "o": Wo_scales}
     bias_in = {"i": bi, "z": bz, "f": bf, "o": bo}
-    gate_func = {"i": ACT.Exp, "z": ACT.Tanh, "f": ACT.Tanh, "o": ACT.Tanh}
-    gate_scale = {"i": 1.0, "z": 1.0, "f": 0.5, "o": 0.5}
+    gate_func = {"i": ACT.Exp, "z": ACT.Tanh, "f": ACT.Tanh}
+    gate_scale = {"i": 1.0, "z": 1.0, "f": 0.5}
 
     def by_row_tile(dram):
         return dram.rearrange("(t p) f -> p t f", p=P)
@@ -74,7 +76,7 @@ def tile_slstmcell_kernel(
     with ExitStack() as ctx:
         ctx.enter_context(tc.manual_schedule())
         keep = ctx.enter_context(tc.tile_pool(name="keep", bufs=1))
-        gate_psum = ctx.enter_context(tc.psum_pool(name="gate_psum", bufs=4))
+        gate_psum = ctx.enter_context(tc.psum_pool(name="gate_psum", bufs=len(GATES)))
         turn_psum = ctx.enter_context(tc.psum_pool(name="turn_psum", bufs=4))
         stage = ctx.enter_context(tc.tile_pool(name="stage", bufs=PASSES))
         acts = ctx.enter_context(tc.tile_pool(name="acts", bufs=2))
@@ -93,8 +95,8 @@ def tile_slstmcell_kernel(
         make_identity(nc, ident[:])
         div_eps = keep.tile([P, 1], F32)
         nc.vector.memset(div_eps[:], DIV_EPS)
-        minus_half = keep.tile([P, 1], F32)
-        nc.vector.memset(minus_half[:], -0.5)
+        ln_eps4 = keep.tile([P, 1], F32)
+        nc.vector.memset(ln_eps4[:], 4.0 * LN_EPS)
 
         w_words = {}
         for gate in GATES:
@@ -104,7 +106,7 @@ def tile_slstmcell_kernel(
         old_m = keep.tile([P, ROW_TILES, H], BF16)
         codes = keep.tile([P, PASSES, B], U32, align_bytes=64)
         code_scales = keep.tile([P, PASSES, B], U8, align_bytes=64)
-        bias_cols = keep.tile([P, 8 * len(GATES)], F32)
+        bias_cols = keep.tile([P, BLOCKS * len(GATES)], F32)
         gamma_all = keep.tile([P, H], BF16)
         beta_all = keep.tile([P, H], BF16)
         x_rows, h_rows = {}, {}
@@ -124,13 +126,12 @@ def tile_slstmcell_kernel(
                     in_=scales_in[gate].rearrange("g (q r) n -> r q g n", r=4)[r].bitcast(I32),
                 )
 
-        def load_weight_columns(pair, some_gates):
+        def load_weight_columns(pair, gate):
             cols = slice(pair * PAIR_F, (pair + 1) * PAIR_F)
-            for gate in some_gates:
-                nc.sync.dma_start(
-                    out=w_words[gate][:, :, cols].bitcast(I32),
-                    in_=words_in[gate].rearrange("g p n t -> p g (n t)").bitcast(I32)[:, :, cols],
-                )
+            nc.sync.dma_start(
+                out=w_words[gate][:, :, cols].bitcast(I32),
+                in_=words_in[gate].rearrange("g p n t -> p g (n t)").bitcast(I32)[:, :, cols],
+            )
 
         def load_old_state(half, part):
             rows = slice(half * HALF_TILES, (half + 1) * HALF_TILES)
@@ -142,18 +143,19 @@ def tile_slstmcell_kernel(
         load_combined(0)
         for a, gate in enumerate(GATES):
             nc.scalar.dma_start(
-                out=bias_rows[8 * a : 8 * a + 8, :],
+                out=bias_rows[BLOCKS * a : BLOCKS * (a + 1), :],
                 in_=bias_in[gate].rearrange("(j f) -> j f", f=P),
             )
         load_combined(1)
         for gate in GATES:
             load_scales(gate)
-            load_weight_columns(0, (gate,))
+            load_weight_columns(0, gate)
         load_old_state(0, 0)
-        load_weight_columns(1, GATES)
-        load_weight_columns(2, GATES)
-        load_old_state(0, 1)
-        load_weight_columns(3, GATES)
+        for pair in range(1, PAIRS):
+            for gate in GATES:
+                load_weight_columns(pair, gate)
+            if pair == PAIRS // 2:
+                load_old_state(0, 1)
         load_old_state(1, 0)
         load_old_state(1, 1)
         nc.sync.dma_start(out=gamma_all[:], in_=ln_gamma.partition_broadcast(P))
@@ -197,21 +199,24 @@ def tile_slstmcell_kernel(
         nc.gpsimd.tensor_copy(out=bias_rows_f32[:], in_=bias_rows[:])
         bias_turned = turn_psum.tile([P, P], F32, tag="turn")
         nc.tensor.transpose(bias_turned[:], bias_rows_f32[:], ident[:])
-        nc.scalar.copy(out=bias_cols[:, 0:16], in_=bias_turned[:, 0:16])
-        nc.scalar.mul(out=bias_cols[:, 16:32], in_=bias_turned[:, 16:32], mul=0.5)
+        whole = BLOCKS * GATES.index("f")
+        nc.scalar.copy(out=bias_cols[:, 0:whole], in_=bias_turned[:, 0:whole])
+        nc.scalar.mul(out=bias_cols[:, whole:], in_=bias_turned[:, whole : BLOCKS * len(GATES)], mul=0.5)
+
         turn_combined(1, (nc.scalar.copy, nc.scalar.copy, nc.scalar.copy))
         quantise_combined(1)
+
         half_bo = keep.tile([P, HALF_TILES, H], BF16)
-        for c in range(H // BN_CHUNK):
-            spread = turn_psum.tile([P, BN_CHUNK], F32, tag="turn")
-            for j in range(BN_CHUNK // P):
-                col = 8 * GATES.index("o") + c * (BN_CHUNK // P) + j
+        for c in range(H // BANK):
+            spread = turn_psum.tile([P, BANK], F32, tag="turn")
+            for j in range(BANK // P):
+                col = BLOCKS * GATES.index("o") + c * (BANK // P) + j
                 nc.tensor.matmul(
                     spread[:, j * P : (j + 1) * P], lhsT=bias_cols[:, col : col + 1].to_broadcast([P, P]),
                     rhs=ident[:], start=True, stop=True,
                 )
             for tt in range(HALF_TILES):
-                nc.scalar.copy(out=half_bo[:, tt, c * BN_CHUNK : (c + 1) * BN_CHUNK], in_=spread[:])
+                nc.scalar.copy(out=half_bo[:, tt, c * BANK : (c + 1) * BANK], in_=spread[:])
 
         new_n, hidden, recip = {}, {}, {}
         for half in range(HALVES):
@@ -219,155 +224,119 @@ def tile_slstmcell_kernel(
             hidden[half] = halves.tile([P, HALF_TILES, H], F32, name="hidden")
             recip[half] = halves.tile([P, HALF_TILES, H], F32, name="recip")
         new_c, new_m = {}, {}
-        act_of, turned_of, mean_var, rstd = {}, {}, {}, {}
+        sums_of, act_of, turned_of, size_of, twice_of, halved_of = {}, {}, {}, {}, {}, {}
 
-        sums_of = {}
-
-        def mx(unit, some_gates=GATES):
+        def mx_passes(unit, gate):
             half, pair = divmod(unit, PAIRS)
-            rows = slice(half * HALF_B, (half + 1) * HALF_B)
-            for gate in some_gates:
-                sums = gate_psum.tile([P, 2, HALF_B], F32, tag="sums")
-                sums_of[unit, gate] = sums
+            sums = gate_psum.tile([P, 2, HALF_B], F32, tag="sums")
+            sums_of[unit, gate] = sums
+            for s in range(2):
                 if gate == "o":
+                    tile_rows = slice((half * HALF_TILES + s) * P, (half * HALF_TILES + s + 1) * P)
                     feats = slice(pair * PAIR_F, (pair + 1) * PAIR_F)
-                    for tt in range(HALF_TILES):
-                        tile_rows = slice((half * HALF_TILES + tt) * P, (half * HALF_TILES + tt + 1) * P)
-                        for g in range(PASSES):
-                            nc.tensor.matmul_mx(
-                                out=sums[:, tt, :],
-                                lhsT=codes[:, g, tile_rows].bitcast(FP8X4),
-                                lhsT_scale=code_scales[:, g, tile_rows],
-                                rhs=w_words[gate][:, g, feats].bitcast(FP8X4),
-                                rhs_scale=planes[gate][:, g, feats],
-                                start=(g == 0),
-                                stop=(g == PASSES - 1),
-                            )
-                    continue
-                for jj in range(2):
-                    block = 2 * pair + jj
-                    feats = slice(block * P, (block + 1) * P)
-                    for g in range(PASSES):
-                        nc.tensor.matmul_mx(
-                            out=sums[:, jj, :],
-                            lhsT=w_words[gate][:, g, feats].bitcast(FP8X4),
-                            lhsT_scale=planes[gate][:, g, feats],
-                            rhs=codes[:, g, rows].bitcast(FP8X4),
-                            rhs_scale=code_scales[:, g, rows],
-                            start=(g == 0),
-                            stop=(g == PASSES - 1),
-                        )
-
-        def act_(unit, some_gates=GATES):
-            half, pair = divmod(unit, PAIRS)
-            act = act_of.setdefault(unit, {})
-            for gate in some_gates:
-                a = GATES.index(gate)
-                sums = sums_of[unit, gate]
-                act[gate] = acts.tile([P, 2, HALF_B], F32, name="act_" + gate)
-                for jj in range(2):
-                    block = 2 * pair + jj
-                    nc.scalar.activation(
-                        out=act[gate][:, jj, :],
-                        in_=sums[:, jj, :],
-                        func=gate_func[gate],
-                        bias=bias_cols[:, 8 * a + block : 8 * a + block + 1],
-                        scale=gate_scale[gate],
+                    still, still_scale, still_cols = codes, code_scales, tile_rows
+                    moving, moving_scale, moving_cols = w_words[gate], planes[gate], feats
+                else:
+                    feats = slice((2 * pair + s) * P, (2 * pair + s + 1) * P)
+                    rows = slice(half * HALF_B, (half + 1) * HALF_B)
+                    still, still_scale, still_cols = w_words[gate], planes[gate], feats
+                    moving, moving_scale, moving_cols = codes, code_scales, rows
+                for g in range(PASSES):
+                    nc.tensor.matmul_mx(
+                        out=sums[:, s, :],
+                        lhsT=still[:, g, still_cols].bitcast(FP8X4),
+                        lhsT_scale=still_scale[:, g, still_cols],
+                        rhs=moving[:, g, moving_cols].bitcast(FP8X4),
+                        rhs_scale=moving_scale[:, g, moving_cols],
+                        start=(g == 0),
+                        stop=(g == PASSES - 1),
                     )
+
+        def activate(unit, gate):
+            pair = unit % PAIRS
+            act = act_of.setdefault(unit, {})
+            act[gate] = acts.tile([P, 2, HALF_B], F32, name="act_" + gate)
+            if gate == "z":
+                act["iz"] = acts.tile([P, 2, HALF_B], F32, name="act_iz")
+            for s in range(2):
+                col = BLOCKS * GATES.index(gate) + 2 * pair + s
+                nc.scalar.activation(
+                    out=act[gate][:, s, :],
+                    in_=sums_of[unit, gate][:, s, :],
+                    func=gate_func[gate],
+                    bias=bias_cols[:, col : col + 1],
+                    scale=gate_scale[gate],
+                )
                 if gate == "z":
-                    act["iz"] = acts.tile([P, 2, HALF_B], F32, name="act_iz")
-                    nc.gpsimd.tensor_tensor(out=act["iz"][:], in0=act["i"][:], in1=act["z"][:], op=ALU.mult)
+                    nc.gpsimd.tensor_tensor(
+                        out=act["iz"][:, s, :], in0=act["i"][:, s, :], in1=act["z"][:, s, :], op=ALU.mult
+                    )
 
-        halved_of = {}
-
-        def add_o(unit):
-            half, pair = divmod(unit, PAIRS)
-            feats = slice(pair * PAIR_F, (pair + 1) * PAIR_F)
+        def add_output_bias(unit):
+            feats = slice((unit % PAIRS) * PAIR_F, (unit % PAIRS + 1) * PAIR_F)
             halved_of[unit] = work.tile([P, HALF_TILES, PAIR_F], F32, name="halved")
             nc.vector.scalar_tensor_tensor(
                 out=halved_of[unit][:], in0=sums_of[unit, "o"][:], scalar=0.5, in1=half_bo[:, :, feats],
                 op0=ALU.mult, op1=ALU.add,
             )
 
-        def tanh_o(unit):
-            act = act_of.setdefault(unit, {})
-            act["o"] = acts.tile([P, 2, HALF_B], F32, name="act_o")
-            nc.scalar.activation(out=act["o"][:], in_=halved_of[unit][:], func=ACT.Tanh)
+        def activate_output(unit):
+            act_of[unit]["o"] = acts.tile([P, HALF_TILES, PAIR_F], F32, name="act_o")
+            nc.scalar.activation(out=act_of[unit]["o"][:], in_=halved_of[unit][:], func=ACT.Tanh)
 
-        def gates(unit):
-            for gate in GATES:
-                mx(unit, (gate,))
-                act_(unit, (gate,))
-
-        def gates_rest(unit):
-            for gate in GATES[1:]:
-                mx(unit, (gate,))
-                act_(unit, (gate,))
-
-        def turn(unit, names=("f", "i", "iz")):
-            turned = turned_of.setdefault(unit, {})
-            for name in names:
-                turned[name] = turn_psum.tile([P, HALF_TILES, PAIR_F], F32, name="turned_" + name, tag="turn")
-                for jj in range(2):
+        def turn(unit):
+            turned_of[unit] = {}
+            for name in TURNED:
+                turned = turn_psum.tile([P, HALF_TILES, PAIR_F], F32, name="turned_" + name, tag="turn")
+                turned_of[unit][name] = turned
+                for s in range(2):
                     for tt in range(HALF_TILES):
                         nc.tensor.transpose(
-                            turned[name][:, tt, jj * P : (jj + 1) * P],
-                            act_of[unit][name][:, jj, tt * P : (tt + 1) * P],
+                            turned[:, tt, s * P : (s + 1) * P],
+                            act_of[unit][name][:, s, tt * P : (tt + 1) * P],
                             ident[:],
                         )
 
-        size_of = {}
-
-        def absz(unit):
+        def magnitude(unit):
             size_of[unit] = work.tile([P, HALF_TILES, PAIR_F], F32, name="size_iz")
             nc.scalar.activation(out=size_of[unit][:], in_=turned_of[unit]["iz"][:], func=ACT.Abs)
 
-        N_FIRST = ("fn2", "fc2", "fm2", "n", "c", "m", "oc")
-
-        def update(unit, order=("fm2", "fc2", "fn2", "m", "c", "n", "oc")):
-            absz(unit)
-            upd(unit, order)
-
-        def upd(unit, order=("fm2", "fc2", "fn2", "m", "c", "n", "oc")):
+        def update(unit, steps):
             half, pair = divmod(unit, PAIRS)
             part, side = divmod(pair, 2)
             turned = turned_of[unit]
             tiles = slice(half * HALF_TILES, (half + 1) * HALF_TILES)
             feats = slice(pair * PAIR_F, (pair + 1) * PAIR_F)
             in_part = slice(side * PAIR_F, (side + 1) * PAIR_F)
-            shape = [P, HALF_TILES, PAIR_F]
-            if side == 0 and order[0] != "oc":
-                new_c[half, part] = work.tile([P, HALF_TILES, PART_F], F32, name="new_c")
-                new_m[half, part] = work.tile([P, HALF_TILES, PART_F], F32, name="new_m")
+            old = {"fm": old_m, "fc": old_c, "fn": old_n}
+            if unit not in twice_of:
+                if side == 0:
+                    new_c[half, part] = work.tile([P, HALF_TILES, PART_F], F32, name="new_c")
+                    new_m[half, part] = work.tile([P, HALF_TILES, PART_F], F32, name="new_m")
+                twice_of[unit] = {}
+                for name in ("fm", "fc", "fn"):
+                    twice_of[unit][name] = work.tile([P, HALF_TILES, PAIR_F], F32, name="twice_" + name)
+            twice = twice_of[unit]
             c_here = new_c[half, part][:, :, in_part]
-            size_iz = size_of[unit]
-            if order[0] != "oc":
-                fm2 = work.tile(shape, F32)
-                fc2 = work.tile(shape, F32)
-                fn2 = work.tile(shape, F32)
-            else:
-                fm2 = fc2 = fn2 = None
-            twice_of = {"fm2": (fm2, old_m), "fc2": (fc2, old_c), "fn2": (fn2, old_n)}
-            for step in order:
-                if step in twice_of:
-                    twice, old = twice_of[step]
+            for step in steps:
+                if step in old:
                     nc.vector.scalar_tensor_tensor(
-                        out=twice[:], in0=turned["f"][:], scalar=1.0, in1=old[:, tiles, feats],
+                        out=twice[step][:], in0=turned["f"][:], scalar=1.0, in1=old[step][:, tiles, feats],
                         op0=ALU.add, op1=ALU.mult,
                     )
                 if step == "m":
                     nc.vector.scalar_tensor_tensor(
-                        out=new_m[half, part][:, :, in_part], in0=fm2[:], scalar=0.5, in1=size_iz[:],
-                        op0=ALU.mult, op1=ALU.max,
+                        out=new_m[half, part][:, :, in_part], in0=twice["fm"][:], scalar=0.5,
+                        in1=size_of[unit][:], op0=ALU.mult, op1=ALU.max,
                     )
                 if step == "c":
                     nc.vector.scalar_tensor_tensor(
-                        out=c_here, in0=fc2[:], scalar=0.5, in1=turned["iz"][:],
+                        out=c_here, in0=twice["fc"][:], scalar=0.5, in1=turned["iz"][:],
                         op0=ALU.mult, op1=ALU.add,
                     )
                 if step == "n":
                     nc.vector.scalar_tensor_tensor(
-                        out=new_n[half][:, :, feats], in0=fn2[:], scalar=0.5, in1=turned["i"][:],
+                        out=new_n[half][:, :, feats], in0=twice["fn"][:], scalar=0.5, in1=turned["i"][:],
                         op0=ALU.mult, op1=ALU.add,
                     )
                 if step == "oc":
@@ -376,9 +345,6 @@ def tile_slstmcell_kernel(
                         op0=ALU.add, op1=ALU.mult,
                     )
 
-        def upd_oc(unit):
-            upd(unit, ("oc",))
-
         def store_state(half, part):
             tiles = slice(half * HALF_TILES, (half + 1) * HALF_TILES)
             feats = slice(part * PART_F, (part + 1) * PART_F)
@@ -386,58 +352,18 @@ def tile_slstmcell_kernel(
             nc.sync.dma_start(out=by_row_tile(out_1)[:, tiles, feats], in_=new_c[half, part][:])
             nc.sync.dma_start(out=by_row_tile(out_2)[:, tiles, feats], in_=new_n[half][:, :, feats])
 
-        def log_normaliser(half, first_pair, pairs):
-            feats = slice(first_pair * PAIR_F, (first_pair + pairs) * PAIR_F)
+        def square_normaliser(unit):
+            half, pair = divmod(unit, PAIRS)
+            feats = slice(pair * PAIR_F, (pair + 1) * PAIR_F)
             nc.scalar.activation(
                 out=recip[half][:, :, feats], in_=new_n[half][:, :, feats], func=ACT.Square, bias=div_eps[:, 0:1]
             )
 
-        def ars(half, first_pair, pairs):
-            feats = slice(first_pair * PAIR_F, (first_pair + pairs) * PAIR_F)
-            nc.scalar.activation(out=recip[half][:, :, feats], in_=recip[half][:, :, feats], func=ACT.Abs_reciprocal_sqrt)
-
-        def rstd_of(half, tt):
-            nc.gpsimd.tensor_tensor(out=rstd[half, tt][:], in0=rstd[half, tt][:], in1=minus_half[:], op=ALU.pow)
-
-        def reciprocal(half, tt):
-            nc.scalar.activation(out=recip[half][:, tt, :], in_=recip[half][:, tt, :], func=ACT.Abs_reciprocal_sqrt)
-
-        def divide(engine, half, tt):
-            row = hidden[half][:, tt, :]
-            engine.tensor_tensor(out=row, in0=row, in1=recip[half][:, tt, :], op=ALU.mult)
-
-        def statistics(half):
-            stats = {}
-            for tt in range(HALF_TILES):
-                row = hidden[half][:, tt, :]
-                stats[tt] = small.tile([P, H // BN_CHUNK, 6], F32, name="stats")
-                for c in range(H // BN_CHUNK):
-                    nc.vector.bn_stats(out=stats[tt][:, c, :], in_=row[:, c * BN_CHUNK : (c + 1) * BN_CHUNK])
-            for tt in range(HALF_TILES):
-                mean_var[half, tt] = small.tile([P, 2], F32, name="mean_var")
-                nc.vector.bn_aggr(out=mean_var[half, tt][:], in_=stats[tt][:].rearrange("p c s -> p (c s)"))
-            for tt in range(HALF_TILES):
-                rstd[half, tt] = small.tile([P, 1], F32, name="rstd")
-                nc.vector.tensor_scalar_add(out=rstd[half, tt][:], in0=mean_var[half, tt][:, 1:2], scalar1=4.0 * LN_EPS)
-
-        def normalise(half):
-            for tt in range(HALF_TILES):
-                row = hidden[half][:, tt, :]
-                nc.vector.scalar_tensor_tensor(
-                    out=row, in0=row, scalar=mean_var[half, tt][:, 0:1], in1=gamma_all[:],
-                    op0=ALU.subtract, op1=ALU.mult,
-                )
-            for tt in range(HALF_TILES):
-                row = hidden[half][:, tt, :]
-                nc.vector.scalar_tensor_tensor(
-                    out=row, in0=row, scalar=rstd[half, tt][:, 0:1], in1=beta_all[:], op0=ALU.mult, op1=ALU.add
-                )
-                nc.sync.dma_start(out=by_row_tile(out_0)[:, half * HALF_TILES + tt, :], in_=row)
+        def reciprocal(squares):
+            nc.scalar.activation(out=squares, in_=squares, func=ACT.Abs_reciprocal_sqrt)
 
         squares = keep.tile([P, H], BF16)
-        minus_mean, total, sum_sq = {}, {}, {}
-        ln_eps4 = keep.tile([P, 1], F32)
-        nc.vector.memset(ln_eps4[:], 4.0 * LN_EPS)
+        total, minus_mean, sum_sq, rstd = {}, {}, {}, {}
 
         def divide_and_sum(half, tt):
             row = hidden[half][:, tt, :]
@@ -465,10 +391,6 @@ def tile_slstmcell_kernel(
                 bias=ln_eps4[:, 0:1],
             )
 
-        def preload_reciprocal_table():
-            scratch = small.tile([P, 1], F32)
-            nc.scalar.activation(out=scratch[:], in_=ln_eps4[:], func=ACT.Abs_reciprocal_sqrt)
-
         def centre(half, tt):
             nc.vector.scalar_tensor_tensor(
                 out=recip[half][:, tt, :], in0=hidden[half][:, tt, :], scalar=minus_mean[half, tt][:, 0:1],
@@ -476,8 +398,8 @@ def tile_slstmcell_kernel(
             )
 
         def scale_and_store(half, tt):
-            for c in range(H // BN_CHUNK):
-                cols = slice(c * BN_CHUNK, (c + 1) * BN_CHUNK)
+            for c in range(H // BANK):
+                cols = slice(c * BANK, (c + 1) * BANK)
                 nc.vector.scalar_tensor_tensor(
                     out=recip[half][:, tt, cols], in0=recip[half][:, tt, cols], scalar=rstd[half, tt][:, 0:1],
                     in1=beta_all[:, cols], op0=ALU.mult, op1=ALU.add,
@@ -486,56 +408,64 @@ def tile_slstmcell_kernel(
                     out=by_row_tile(out_0)[:, half * HALF_TILES + tt, cols], in_=recip[half][:, tt, cols]
                 )
 
+        def statistics(half):
+            negative_mean(half, 0)
+            squared_deviations(half, 0)
+            negative_mean(half, 1)
+            inverse_deviation(half, 0)
+            squared_deviations(half, 1)
+            inverse_deviation(half, 1)
+
         for gate in ("i", "z", "f"):
-            mx(0, (gate,)); act_(0, (gate,))
-        mx(0, ("o",)); add_o(0); tanh_o(0)
-        started = set()
+            mx_passes(0, gate)
+            activate(0, gate)
+        mx_passes(0, "o")
+        add_output_bias(0)
+        activate_output(0)
         for unit in range(UNITS):
             half, pair = divmod(unit, PAIRS)
             last = unit == UNITS - 1
             turn(unit)
             if last:
-                preload_reciprocal_table()
-            absz(unit)
+                scratch = small.tile([P, 1], F32)
+                nc.scalar.activation(out=scratch[:], in_=ln_eps4[:], func=ACT.Abs_reciprocal_sqrt)
+            magnitude(unit)
             if last:
-                reciprocal(0, 0); reciprocal(0, 1)
-            if not last:
-                for gate in ("i", "z", "f"):
-                    if (unit + 1, gate) not in started:
-                        mx(unit + 1, (gate,)); act_(unit + 1, (gate,))
-                mx(unit + 1, ("o",))
-            if last:
-                upd(unit, ("fn2", "fc2", "fm2", "n", "c", "m"))
+                for tt in range(HALF_TILES):
+                    reciprocal(recip[0][:, tt, :])
+                update(unit, ("fn", "fc", "fm", "n", "c", "m"))
             else:
-                upd(unit, ("fm2", "fc2", "fn2", "m", "c", "n"))
-                add_o(unit + 1)
-            upd_oc(unit)
+                for gate in ("i", "z", "f") if unit == 0 else ("z", "f"):
+                    mx_passes(unit + 1, gate)
+                    activate(unit + 1, gate)
+                mx_passes(unit + 1, "o")
+                update(unit, ("fm", "fc", "fn", "m", "c", "n"))
+                add_output_bias(unit + 1)
+            update(unit, ("oc",))
             if unit > 0:
-                log_normaliser((unit - 1) // PAIRS, (unit - 1) % PAIRS, 1)
+                square_normaliser(unit - 1)
             if unit + 2 < UNITS:
-                mx(unit + 2, ("i",)); act_(unit + 2, ("i",)); started.add((unit + 2, "i"))
+                mx_passes(unit + 2, "i")
+                activate(unit + 2, "i")
             if not last:
-                tanh_o(unit + 1)
+                activate_output(unit + 1)
             if pair % 2 == 1:
                 store_state(half, pair // 2)
-        ars(1, 0, 3)
-        divide_and_sum(0, 0); divide_and_sum(0, 1)
-        negative_mean(0, 0)
-        squared_deviations(0, 0)
-        negative_mean(0, 1)
-        inverse_deviation(0, 0)
-        squared_deviations(0, 1)
-        inverse_deviation(0, 1)
-        centre(0, 0); centre(0, 1)
-        log_normaliser(1, 3, 1)
-        ars(1, 3, 1)
-        scale_and_store(0, 0); scale_and_store(0, 1)
-        divide_and_sum(1, 0); divide_and_sum(1, 1)
-        negative_mean(1, 0)
-        squared_deviations(1, 0)
-        negative_mean(1, 1)
-        inverse_deviation(1, 0)
-        squared_deviations(1, 1)
-        inverse_deviation(1, 1)
-        centre(1, 0); centre(1, 1)
-        scale_and_store(1, 0); scale_and_store(1, 1)
+
+        reciprocal(recip[1][:, :, 0 : (PAIRS - 1) * PAIR_F])
+        for tt in range(HALF_TILES):
+            divide_and_sum(0, tt)
+        statistics(0)
+        for tt in range(HALF_TILES):
+            centre(0, tt)
+        square_normaliser(UNITS - 1)
+        reciprocal(recip[1][:, :, (PAIRS - 1) * PAIR_F : H])
+        for tt in range(HALF_TILES):
+            scale_and_store(0, tt)
+        for tt in range(HALF_TILES):
+            divide_and_sum(1, tt)
+        statistics(1)
+        for tt in range(HALF_TILES):
+            centre(1, tt)
+        for tt in range(HALF_TILES):
+            scale_and_store(1, tt)

@@ -82,6 +82,8 @@ def tile_slstmcell_kernel(
         acts = ctx.enter_context(tc.tile_pool(name="acts", bufs=2))
         work = ctx.enter_context(tc.tile_pool(name="work", bufs=2))
         halves = ctx.enter_context(tc.tile_pool(name="halves", bufs=HALVES))
+        quarters = ctx.enter_context(tc.tile_pool(name="quarters", bufs=2 * HALVES))
+        products = ctx.enter_context(tc.tile_pool(name="products", bufs=1))
         small = ctx.enter_context(tc.tile_pool(name="small", bufs=ROW_TILES))
 
         planes = {}
@@ -151,13 +153,13 @@ def tile_slstmcell_kernel(
             load_scales(gate)
             load_weight_columns(0, gate)
         load_old_state(0, 0)
+        load_old_state(1, 0)
         for pair in range(1, PAIRS):
             for gate in GATES:
                 load_weight_columns(pair, gate)
             if pair == PAIRS // 2:
                 load_old_state(0, 1)
-        load_old_state(1, 0)
-        load_old_state(1, 1)
+                load_old_state(1, 1)
         nc.sync.dma_start(out=gamma_all[:], in_=ln_gamma.partition_broadcast(P))
         nc.sync.dma_start(out=beta_all[:], in_=ln_beta.partition_broadcast(P))
 
@@ -227,7 +229,7 @@ def tile_slstmcell_kernel(
         sums_of, act_of, turned_of, size_of, twice_of, halved_of = {}, {}, {}, {}, {}, {}
 
         def mx_passes(unit, gate):
-            half, pair = divmod(unit, PAIRS)
+            pair, half = divmod(unit, HALVES)
             sums = gate_psum.tile([P, 2, HALF_B], F32, tag="sums")
             sums_of[unit, gate] = sums
             for s in range(2):
@@ -253,7 +255,7 @@ def tile_slstmcell_kernel(
                     )
 
         def activate(unit, gate):
-            pair = unit % PAIRS
+            pair = unit // HALVES
             act = act_of.setdefault(unit, {})
             act[gate] = acts.tile([P, 2, HALF_B], F32, name="act_" + gate)
             if gate == "z":
@@ -273,7 +275,8 @@ def tile_slstmcell_kernel(
                     )
 
         def add_output_bias(unit):
-            feats = slice((unit % PAIRS) * PAIR_F, (unit % PAIRS + 1) * PAIR_F)
+            pair = unit // HALVES
+            feats = slice(pair * PAIR_F, (pair + 1) * PAIR_F)
             halved_of[unit] = work.tile([P, HALF_TILES, PAIR_F], F32, name="halved")
             nc.vector.scalar_tensor_tensor(
                 out=halved_of[unit][:], in0=sums_of[unit, "o"][:], scalar=0.5, in1=half_bo[:, :, feats],
@@ -302,7 +305,7 @@ def tile_slstmcell_kernel(
             nc.scalar.activation(out=size_of[unit][:], in_=turned_of[unit]["iz"][:], func=ACT.Abs)
 
         def update(unit, steps):
-            half, pair = divmod(unit, PAIRS)
+            pair, half = divmod(unit, HALVES)
             part, side = divmod(pair, 2)
             turned = turned_of[unit]
             tiles = slice(half * HALF_TILES, (half + 1) * HALF_TILES)
@@ -311,11 +314,11 @@ def tile_slstmcell_kernel(
             old = {"fm": old_m, "fc": old_c, "fn": old_n}
             if unit not in twice_of:
                 if side == 0:
-                    new_c[half, part] = work.tile([P, HALF_TILES, PART_F], F32, name="new_c")
-                    new_m[half, part] = work.tile([P, HALF_TILES, PART_F], F32, name="new_m")
+                    new_c[half, part] = quarters.tile([P, HALF_TILES, PART_F], F32, name="new_c")
+                    new_m[half, part] = quarters.tile([P, HALF_TILES, PART_F], F32, name="new_m")
                 twice_of[unit] = {}
                 for name in ("fm", "fc", "fn"):
-                    twice_of[unit][name] = work.tile([P, HALF_TILES, PAIR_F], F32, name="twice_" + name)
+                    twice_of[unit][name] = products.tile([P, HALF_TILES, PAIR_F], F32, name="twice_" + name)
             twice = twice_of[unit]
             c_here = new_c[half, part][:, :, in_part]
             for step in steps:
@@ -353,7 +356,7 @@ def tile_slstmcell_kernel(
             nc.sync.dma_start(out=by_row_tile(out_2)[:, tiles, feats], in_=new_n[half][:, :, feats])
 
         def square_normaliser(unit):
-            half, pair = divmod(unit, PAIRS)
+            pair, half = divmod(unit, HALVES)
             feats = slice(pair * PAIR_F, (pair + 1) * PAIR_F)
             nc.scalar.activation(
                 out=recip[half][:, :, feats], in_=new_n[half][:, :, feats], func=ACT.Square, bias=div_eps[:, 0:1]
@@ -422,8 +425,10 @@ def tile_slstmcell_kernel(
         mx_passes(0, "o")
         add_output_bias(0)
         activate_output(0)
+        mx_passes(1, "i")
+        activate(1, "i")
         for unit in range(UNITS):
-            half, pair = divmod(unit, PAIRS)
+            pair, half = divmod(unit, HALVES)
             last = unit == UNITS - 1
             turn(unit)
             if last:
@@ -431,18 +436,19 @@ def tile_slstmcell_kernel(
                 nc.scalar.activation(out=scratch[:], in_=ln_eps4[:], func=ACT.Abs_reciprocal_sqrt)
             magnitude(unit)
             if last:
+                square_normaliser(unit - 1)
                 for tt in range(HALF_TILES):
                     reciprocal(recip[0][:, tt, :])
                 update(unit, ("fn", "fc", "fm", "n", "c", "m"))
             else:
-                for gate in ("i", "z", "f") if unit == 0 else ("z", "f"):
+                for gate in ("z", "f"):
                     mx_passes(unit + 1, gate)
                     activate(unit + 1, gate)
                 mx_passes(unit + 1, "o")
                 update(unit, ("fm", "fc", "fn", "m", "c", "n"))
                 add_output_bias(unit + 1)
             update(unit, ("oc",))
-            if unit > 0:
+            if 0 < unit < UNITS - 1:
                 square_normaliser(unit - 1)
             if unit + 2 < UNITS:
                 mx_passes(unit + 2, "i")

@@ -32,6 +32,7 @@ BANK = 512
 BLOCKS = H // P
 
 GATES = ("i", "z", "f", "o")
+BIAS_ORDER = ("i", "z", "f")
 TURNED = ("f", "i", "iz")
 
 FLOPS = 2 * B * D * 4 * H
@@ -86,19 +87,24 @@ def tile_slstmcell_kernel(
         products = ctx.enter_context(tc.tile_pool(name="products", bufs=1))
         small = ctx.enter_context(tc.tile_pool(name="small", bufs=ROW_TILES))
 
-        planes = {}
         bias_rows = keep.tile([P, P], BF16)
+        nc.gpsimd.memset(bias_rows[:], 0.0)
+        ident = keep.tile([P, P], F32)
+        make_identity(nc, ident[:])
+        ident_bf16 = keep.tile([P, P], BF16)
+        nc.gpsimd.tensor_copy(out=ident_bf16[:], in_=ident[:])
+        bo_row = keep.tile([P, H], BF16)
+        nc.gpsimd.memset(bo_row[:], 0.0)
+        beta_row = keep.tile([P, H], BF16)
+        nc.gpsimd.memset(beta_row[:], 0.0)
+        ones = keep.tile([P, P], BF16)
+        nc.gpsimd.memset(ones[:], 1.0)
+        planes = {}
         for gate in GATES:
             planes[gate] = keep.tile([P, PASSES, H], U8, name="planes_" + gate, align_bytes=64)
             nc.vector.memset(planes[gate][:].rearrange("p g n -> p (g n)").bitcast(I32), 0)
-            if gate == GATES[0]:
-                nc.vector.memset(bias_rows[:], 0.0)
-        ident = keep.tile([P, P], F32)
-        make_identity(nc, ident[:])
-        div_eps = keep.tile([P, 1], F32)
-        nc.vector.memset(div_eps[:], DIV_EPS)
-        ln_eps4 = keep.tile([P, 1], F32)
-        nc.vector.memset(ln_eps4[:], 4.0 * LN_EPS)
+        ln_eps = keep.tile([P, 1], F32)
+        nc.vector.memset(ln_eps[:], LN_EPS)
 
         w_words = {}
         for gate in GATES:
@@ -108,7 +114,7 @@ def tile_slstmcell_kernel(
         old_m = keep.tile([P, ROW_TILES, H], BF16)
         codes = keep.tile([P, PASSES, B], U32, align_bytes=64)
         code_scales = keep.tile([P, PASSES, B], U8, align_bytes=64)
-        bias_cols = keep.tile([P, BLOCKS * len(GATES)], F32)
+        bias_cols = keep.tile([P, BLOCKS * len(BIAS_ORDER)], F32)
         gamma_all = keep.tile([P, H], BF16)
         beta_all = keep.tile([P, H], BF16)
         x_rows, h_rows = {}, {}
@@ -138,21 +144,24 @@ def tile_slstmcell_kernel(
         def load_old_state(half, part):
             rows = slice(half * HALF_TILES, (half + 1) * HALF_TILES)
             feats = slice(part * PART_F, (part + 1) * PART_F)
-            nc.sync.dma_start(out=old_m[:, rows, feats], in_=by_row_tile(m_prev)[:, rows, feats])
-            nc.sync.dma_start(out=old_c[:, rows, feats], in_=by_row_tile(c_prev)[:, rows, feats])
             nc.sync.dma_start(out=old_n[:, rows, feats], in_=by_row_tile(n_prev)[:, rows, feats])
+            nc.sync.dma_start(out=old_c[:, rows, feats], in_=by_row_tile(c_prev)[:, rows, feats])
+            nc.sync.dma_start(out=old_m[:, rows, feats], in_=by_row_tile(m_prev)[:, rows, feats])
 
-        load_combined(0)
-        for a, gate in enumerate(GATES):
-            nc.scalar.dma_start(
+        for a, name in enumerate(BIAS_ORDER):
+            nc.sync.dma_start(
                 out=bias_rows[BLOCKS * a : BLOCKS * (a + 1), :],
-                in_=bias_in[gate].rearrange("(j f) -> j f", f=P),
+                in_=bias_in[name].rearrange("(j f) -> j f", f=P),
             )
-        load_combined(1)
-        for gate in GATES:
-            load_scales(gate)
+        load_combined(0)
+        for gate in ("i", "z", "f"):
             load_weight_columns(0, gate)
+            load_scales(gate)
+        load_combined(1)
         load_old_state(0, 0)
+        load_weight_columns(0, "o")
+        load_scales("o")
+        nc.sync.dma_start(out=bo_row[0:1, :], in_=bo.rearrange("(r f) -> r f", r=1))
         load_old_state(1, 0)
         for pair in range(1, PAIRS):
             for gate in GATES:
@@ -162,6 +171,7 @@ def tile_slstmcell_kernel(
                 load_old_state(1, 1)
         nc.sync.dma_start(out=gamma_all[:], in_=ln_gamma.partition_broadcast(P))
         nc.sync.dma_start(out=beta_all[:], in_=ln_beta.partition_broadcast(P))
+        nc.sync.dma_start(out=beta_row[0:1, :], in_=ln_beta.rearrange("(r f) -> r f", r=1))
 
         grouped = {}
 
@@ -194,39 +204,32 @@ def tile_slstmcell_kernel(
                     in_=grouped[half, g][:].rearrange("p b t -> p (b t)"),
                 )
 
-        turn_combined(0, (nc.vector.tensor_copy, nc.scalar.copy, nc.vector.tensor_copy))
-        quantise_combined(0)
+        exp_minus_bo = keep.tile([P, H], F32)
 
-        bias_rows_f32 = keep.tile([P, P], F32)
-        nc.gpsimd.tensor_copy(out=bias_rows_f32[:], in_=bias_rows[:])
-        bias_turned = turn_psum.tile([P, P], F32, tag="turn")
-        nc.tensor.transpose(bias_turned[:], bias_rows_f32[:], ident[:])
-        whole = BLOCKS * GATES.index("f")
-        nc.scalar.copy(out=bias_cols[:, 0:whole], in_=bias_turned[:, 0:whole])
-        nc.scalar.mul(out=bias_cols[:, whole:], in_=bias_turned[:, whole : BLOCKS * len(GATES)], mul=0.5)
+        def turn_biases():
+            bias_turned = turn_psum.tile([P, P], BF16, tag="turn")
+            nc.tensor.transpose(bias_turned[:], bias_rows[:], ident_bf16[:])
+            whole = BLOCKS * BIAS_ORDER.index("f")
+            nc.scalar.copy(out=bias_cols[:, 0:whole], in_=bias_turned[:, 0:whole])
+            nc.scalar.mul(out=bias_cols[:, whole:], in_=bias_turned[:, whole : BLOCKS * len(BIAS_ORDER)], mul=0.5)
 
-        turn_combined(1, (nc.scalar.copy, nc.scalar.copy, nc.scalar.copy))
-        quantise_combined(1)
-
-        half_bo = keep.tile([P, HALF_TILES, H], BF16)
-        for c in range(H // BANK):
-            spread = turn_psum.tile([P, BANK], F32, tag="turn")
-            for j in range(BANK // P):
-                col = BLOCKS * GATES.index("o") + c * (BANK // P) + j
-                nc.tensor.matmul(
-                    spread[:, j * P : (j + 1) * P], lhsT=bias_cols[:, col : col + 1].to_broadcast([P, P]),
-                    rhs=ident[:], start=True, stop=True,
+        def spread_output_bias():
+            for c in range(H // BANK):
+                cols = slice(c * BANK, (c + 1) * BANK)
+                spread = gate_psum.tile([P, BANK], F32, tag="sums")
+                nc.tensor.matmul(spread[:], lhsT=ones[:], rhs=bo_row[:, cols], start=True, stop=True)
+                nc.scalar.activation(
+                    out=exp_minus_bo[:, cols], in_=spread[:], func=ACT.Exp, scale=-1.0
                 )
-            for tt in range(HALF_TILES):
-                nc.scalar.copy(out=half_bo[:, tt, c * BANK : (c + 1) * BANK], in_=spread[:])
 
-        new_n, hidden, recip = {}, {}, {}
+        new_n, new_c, hidden, recip = {}, {}, {}, {}
         for half in range(HALVES):
+            new_c[half] = halves.tile([P, HALF_TILES, H], F32, name="new_c")
             new_n[half] = halves.tile([P, HALF_TILES, H], F32, name="new_n")
             hidden[half] = halves.tile([P, HALF_TILES, H], F32, name="hidden")
             recip[half] = halves.tile([P, HALF_TILES, H], F32, name="recip")
-        new_c, new_m = {}, {}
-        sums_of, act_of, turned_of, size_of, twice_of, halved_of = {}, {}, {}, {}, {}, {}
+        new_m = {}
+        sums_of, act_of, turned_of, size_of, twice_of = {}, {}, {}, {}, {}
 
         def mx_passes(unit, gate):
             pair, half = divmod(unit, HALVES)
@@ -261,7 +264,7 @@ def tile_slstmcell_kernel(
             if gate == "z":
                 act["iz"] = acts.tile([P, 2, HALF_B], F32, name="act_iz")
             for s in range(2):
-                col = BLOCKS * GATES.index(gate) + 2 * pair + s
+                col = BLOCKS * BIAS_ORDER.index(gate) + 2 * pair + s
                 nc.scalar.activation(
                     out=act[gate][:, s, :],
                     in_=sums_of[unit, gate][:, s, :],
@@ -274,18 +277,19 @@ def tile_slstmcell_kernel(
                         out=act["iz"][:, s, :], in0=act["i"][:, s, :], in1=act["z"][:, s, :], op=ALU.mult
                     )
 
-        def add_output_bias(unit):
+        def activate_output(unit):
             pair = unit // HALVES
             feats = slice(pair * PAIR_F, (pair + 1) * PAIR_F)
-            halved_of[unit] = work.tile([P, HALF_TILES, PAIR_F], F32, name="halved")
-            nc.vector.scalar_tensor_tensor(
-                out=halved_of[unit][:], in0=sums_of[unit, "o"][:], scalar=0.5, in1=half_bo[:, :, feats],
-                op0=ALU.mult, op1=ALU.add,
+            inverse = acts.tile([P, HALF_TILES, PAIR_F], F32, name="inverse_o")
+            act_of[unit]["inverse_o"] = inverse
+            nc.scalar.activation(out=inverse[:], in_=sums_of[unit, "o"][:], func=ACT.Exp, scale=-1.0)
+            for tt in range(HALF_TILES):
+                nc.gpsimd.tensor_tensor(
+                    out=inverse[:, tt, :], in0=inverse[:, tt, :], in1=exp_minus_bo[:, feats], op=ALU.mult
+                )
+            nc.gpsimd.tensor_scalar(
+                out=inverse[:], in0=inverse[:], scalar1=1.0, scalar2=1.0, op0=ALU.add, op1=ALU.mult
             )
-
-        def activate_output(unit):
-            act_of[unit]["o"] = acts.tile([P, HALF_TILES, PAIR_F], F32, name="act_o")
-            nc.scalar.activation(out=act_of[unit]["o"][:], in_=halved_of[unit][:], func=ACT.Tanh)
 
         def turn(unit):
             turned_of[unit] = {}
@@ -314,13 +318,12 @@ def tile_slstmcell_kernel(
             old = {"fm": old_m, "fc": old_c, "fn": old_n}
             if unit not in twice_of:
                 if side == 0:
-                    new_c[half, part] = quarters.tile([P, HALF_TILES, PART_F], F32, name="new_c")
                     new_m[half, part] = quarters.tile([P, HALF_TILES, PART_F], F32, name="new_m")
                 twice_of[unit] = {}
                 for name in ("fm", "fc", "fn"):
                     twice_of[unit][name] = products.tile([P, HALF_TILES, PAIR_F], F32, name="twice_" + name)
             twice = twice_of[unit]
-            c_here = new_c[half, part][:, :, in_part]
+            c_here = new_c[half][:, :, feats]
             for step in steps:
                 if step in old:
                     nc.vector.scalar_tensor_tensor(
@@ -342,37 +345,35 @@ def tile_slstmcell_kernel(
                         out=new_n[half][:, :, feats], in0=twice["fn"][:], scalar=0.5, in1=turned["i"][:],
                         op0=ALU.mult, op1=ALU.add,
                     )
-                if step == "oc":
+                if step == "d":
                     nc.vector.scalar_tensor_tensor(
-                        out=hidden[half][:, :, feats], in0=act_of[unit]["o"][:], scalar=1.0, in1=c_here,
-                        op0=ALU.add, op1=ALU.mult,
+                        out=recip[half][:, :, feats], in0=new_n[half][:, :, feats], scalar=DIV_EPS,
+                        in1=act_of[unit]["inverse_o"][:], op0=ALU.add, op1=ALU.mult,
                     )
 
         def store_state(half, part):
             tiles = slice(half * HALF_TILES, (half + 1) * HALF_TILES)
             feats = slice(part * PART_F, (part + 1) * PART_F)
             nc.sync.dma_start(out=by_row_tile(out_3)[:, tiles, feats], in_=new_m[half, part][:])
-            nc.sync.dma_start(out=by_row_tile(out_1)[:, tiles, feats], in_=new_c[half, part][:])
+            nc.sync.dma_start(out=by_row_tile(out_1)[:, tiles, feats], in_=new_c[half][:, :, feats])
             nc.sync.dma_start(out=by_row_tile(out_2)[:, tiles, feats], in_=new_n[half][:, :, feats])
 
-        def square_normaliser(unit):
+        def square_divisor(unit):
             pair, half = divmod(unit, HALVES)
             feats = slice(pair * PAIR_F, (pair + 1) * PAIR_F)
-            nc.scalar.activation(
-                out=recip[half][:, :, feats], in_=new_n[half][:, :, feats], func=ACT.Square, bias=div_eps[:, 0:1]
-            )
+            nc.scalar.activation(out=recip[half][:, :, feats], in_=recip[half][:, :, feats], func=ACT.Square)
 
         def reciprocal(squares):
             nc.scalar.activation(out=squares, in_=squares, func=ACT.Abs_reciprocal_sqrt)
 
         squares = keep.tile([P, H], BF16)
-        total, minus_mean, sum_sq, rstd = {}, {}, {}, {}
+        total, minus_mean, sum_sq, rstd, diagonal, scaled_of = {}, {}, {}, {}, {}, {}
 
         def divide_and_sum(half, tt):
-            row = hidden[half][:, tt, :]
             total[half, tt] = small.tile([P, 1], F32, name="total")
             nc.vector.scalar_tensor_tensor(
-                out=row, in0=row, scalar=1.0, in1=recip[half][:, tt, :], op0=ALU.mult, op1=ALU.mult,
+                out=hidden[half][:, tt, :], in0=new_c[half][:, tt, :], scalar=1.0, in1=recip[half][:, tt, :],
+                op0=ALU.mult, op1=ALU.mult,
                 accum_out=total[half, tt][:],
             )
 
@@ -391,7 +392,7 @@ def tile_slstmcell_kernel(
             rstd[half, tt] = small.tile([P, 1], F32, name="rstd")
             nc.scalar.activation(
                 out=rstd[half, tt][:], in_=sum_sq[half, tt][:], func=ACT.Abs_reciprocal_sqrt, scale=1.0 / H,
-                bias=ln_eps4[:, 0:1],
+                bias=ln_eps[:, 0:1],
             )
 
         def centre(half, tt):
@@ -411,67 +412,111 @@ def tile_slstmcell_kernel(
                     out=by_row_tile(out_0)[:, half * HALF_TILES + tt, cols], in_=recip[half][:, tt, cols]
                 )
 
-        def statistics(half):
-            negative_mean(half, 0)
-            squared_deviations(half, 0)
-            negative_mean(half, 1)
-            inverse_deviation(half, 0)
-            squared_deviations(half, 1)
-            inverse_deviation(half, 1)
+        def deviation_on_diagonal(half, tt):
+            diagonal[half, tt] = small.tile([P, P], F32, name="diagonal")
+            nc.scalar.activation(
+                out=diagonal[half, tt][:], in_=ident[:], func=ACT.Copy, scale=rstd[half, tt][:, 0:1]
+            )
 
-        for gate in ("i", "z", "f"):
+        def scale_on_tensor(half, tt):
+            for c in range(H // BANK):
+                cols = slice(c * BANK, (c + 1) * BANK)
+                scaled = gate_psum.tile([P, BANK], F32, name="scaled", tag="sums")
+                scaled_of[half, tt, c] = scaled
+                nc.tensor.matmul(scaled[:], lhsT=ones[:], rhs=beta_row[:, cols], start=True, stop=False)
+                nc.tensor.matmul(
+                    scaled[:], lhsT=diagonal[half, tt][:], rhs=recip[half][:, tt, cols], start=False, stop=True
+                )
+
+        def store_scaled(half, tt):
+            for c in range(H // BANK):
+                cols = slice(c * BANK, (c + 1) * BANK)
+                nc.scalar.copy(out=hidden[half][:, tt, cols], in_=scaled_of[half, tt, c][:])
+                nc.scalar.dma_start(
+                    out=by_row_tile(out_0)[:, half * HALF_TILES + tt, cols], in_=hidden[half][:, tt, cols]
+                )
+
+        turn_combined(0, (nc.vector.tensor_copy, nc.scalar.copy, nc.vector.tensor_copy))
+        quantise_combined(0)
+        turn_biases()
+        mx_passes(0, "i")
+        activate(0, "i")
+        for gate in ("z", "f"):
             mx_passes(0, gate)
             activate(0, gate)
-        mx_passes(0, "o")
-        add_output_bias(0)
-        activate_output(0)
-        mx_passes(1, "i")
-        activate(1, "i")
+        turn_combined(1, (nc.vector.tensor_copy,) * PASSES)
+        quantise_combined(1)
+        early, late = slice(0, H - PAIR_F), slice(H - PAIR_F, H)
         for unit in range(UNITS):
             pair, half = divmod(unit, HALVES)
             last = unit == UNITS - 1
             turn(unit)
             if last:
                 scratch = small.tile([P, 1], F32)
-                nc.scalar.activation(out=scratch[:], in_=ln_eps4[:], func=ACT.Abs_reciprocal_sqrt)
-            magnitude(unit)
+                nc.scalar.activation(out=scratch[:], in_=ln_eps[:], func=ACT.Abs_reciprocal_sqrt)
+                reciprocal(recip[0][:, 0, early])
+            else:
+                magnitude(unit)
+            if unit == 0:
+                spread_output_bias()
+                mx_passes(0, "o")
+                activate_output(0)
+                mx_passes(1, "i")
+                activate(1, "i")
             if last:
-                square_normaliser(unit - 1)
-                for tt in range(HALF_TILES):
-                    reciprocal(recip[0][:, tt, :])
-                update(unit, ("fn", "fc", "fm", "n", "c", "m"))
+                update(unit, ("fn", "fc"))
+                update(unit - 1, ("d",))
+                square_divisor(unit - 1)
+                reciprocal(recip[0][:, 0, late])
+                reciprocal(recip[0][:, 1, early])
+                reciprocal(recip[0][:, 1, late])
+                update(unit, ("c", "n", "fm", "d"))
+                magnitude(unit)
+                square_divisor(unit)
+                divide_and_sum(0, 0)
+                update(unit, ("m",))
             else:
                 for gate in ("z", "f"):
                     mx_passes(unit + 1, gate)
                     activate(unit + 1, gate)
                 mx_passes(unit + 1, "o")
-                update(unit, ("fm", "fc", "fn", "m", "c", "n"))
-                add_output_bias(unit + 1)
-            update(unit, ("oc",))
-            if 0 < unit < UNITS - 1:
-                square_normaliser(unit - 1)
+                activate_output(unit + 1)
+                update(unit, ("fn", "fc", "fm"))
+                if unit > 0:
+                    update(unit - 1, ("d",))
+                update(unit, ("n", "c", "m"))
             if unit + 2 < UNITS:
                 mx_passes(unit + 2, "i")
                 activate(unit + 2, "i")
-            if not last:
-                activate_output(unit + 1)
+            if 0 < unit < UNITS - 1:
+                square_divisor(unit - 1)
             if pair % 2 == 1:
                 store_state(half, pair // 2)
 
-        reciprocal(recip[1][:, :, 0 : (PAIRS - 1) * PAIR_F])
-        for tt in range(HALF_TILES):
-            divide_and_sum(0, tt)
-        statistics(0)
+        negative_mean(0, 0)
+        squared_deviations(0, 0)
+        divide_and_sum(0, 1)
+        negative_mean(0, 1)
+        inverse_deviation(0, 0)
+        squared_deviations(0, 1)
+        deviation_on_diagonal(0, 0)
+        inverse_deviation(0, 1)
+        reciprocal(recip[1][:, 0, :])
+        deviation_on_diagonal(0, 1)
+        reciprocal(recip[1][:, 1, :])
         for tt in range(HALF_TILES):
             centre(0, tt)
-        square_normaliser(UNITS - 1)
-        reciprocal(recip[1][:, :, (PAIRS - 1) * PAIR_F : H])
-        for tt in range(HALF_TILES):
-            scale_and_store(0, tt)
-        for tt in range(HALF_TILES):
-            divide_and_sum(1, tt)
-        statistics(1)
+            scale_on_tensor(0, tt)
+        divide_and_sum(1, 0)
+        negative_mean(1, 0)
+        squared_deviations(1, 0)
+        divide_and_sum(1, 1)
+        negative_mean(1, 1)
+        inverse_deviation(1, 0)
+        store_scaled(0, 0)
+        squared_deviations(1, 1)
+        inverse_deviation(1, 1)
+        store_scaled(0, 1)
         for tt in range(HALF_TILES):
             centre(1, tt)
-        for tt in range(HALF_TILES):
             scale_and_store(1, tt)

@@ -83,7 +83,7 @@ def tile_slstmcell_kernel(
         acts = ctx.enter_context(tc.tile_pool(name="acts", bufs=2))
         work = ctx.enter_context(tc.tile_pool(name="work", bufs=2))
         halves = ctx.enter_context(tc.tile_pool(name="halves", bufs=HALVES))
-        quarters = ctx.enter_context(tc.tile_pool(name="quarters", bufs=2 * HALVES))
+        quarters = ctx.enter_context(tc.tile_pool(name="quarters", bufs=3))
         products = ctx.enter_context(tc.tile_pool(name="products", bufs=1))
         small = ctx.enter_context(tc.tile_pool(name="small", bufs=ROW_TILES))
 
@@ -103,8 +103,10 @@ def tile_slstmcell_kernel(
         for gate in GATES:
             planes[gate] = keep.tile([P, PASSES, H], U8, name="planes_" + gate, align_bytes=64)
             nc.vector.memset(planes[gate][:].rearrange("p g n -> p (g n)").bitcast(I32), 0)
+        div_eps = keep.tile([P, 1], F32)
+        nc.vector.memset(div_eps[:], DIV_EPS)
         ln_eps = keep.tile([P, 1], F32)
-        nc.vector.memset(ln_eps[:], LN_EPS)
+        nc.vector.memset(ln_eps[:], 4.0 * LN_EPS)
 
         w_words = {}
         for gate in GATES:
@@ -204,7 +206,7 @@ def tile_slstmcell_kernel(
                     in_=grouped[half, g][:].rearrange("p b t -> p (b t)"),
                 )
 
-        exp_minus_bo = keep.tile([P, H], F32)
+        half_bo = keep.tile([P, H], BF16)
 
         def turn_biases():
             bias_turned = turn_psum.tile([P, P], BF16, tag="turn")
@@ -218,9 +220,7 @@ def tile_slstmcell_kernel(
                 cols = slice(c * BANK, (c + 1) * BANK)
                 spread = gate_psum.tile([P, BANK], F32, tag="sums")
                 nc.tensor.matmul(spread[:], lhsT=ones[:], rhs=bo_row[:, cols], start=True, stop=True)
-                nc.scalar.activation(
-                    out=exp_minus_bo[:, cols], in_=spread[:], func=ACT.Exp, scale=-1.0
-                )
+                nc.scalar.mul(out=half_bo[:, cols], in_=spread[:], mul=0.5)
 
         new_n, new_c, hidden, recip = {}, {}, {}, {}
         for half in range(HALVES):
@@ -229,7 +229,7 @@ def tile_slstmcell_kernel(
             hidden[half] = halves.tile([P, HALF_TILES, H], F32, name="hidden")
             recip[half] = halves.tile([P, HALF_TILES, H], F32, name="recip")
         new_m = {}
-        sums_of, act_of, turned_of, size_of, twice_of = {}, {}, {}, {}, {}
+        sums_of, act_of, turned_of, size_of, twice_of, halved_of = {}, {}, {}, {}, {}, {}
 
         def mx_passes(unit, gate):
             pair, half = divmod(unit, HALVES)
@@ -277,19 +277,19 @@ def tile_slstmcell_kernel(
                         out=act["iz"][:, s, :], in0=act["i"][:, s, :], in1=act["z"][:, s, :], op=ALU.mult
                     )
 
-        def activate_output(unit):
+        def add_output_bias(unit):
             pair = unit // HALVES
             feats = slice(pair * PAIR_F, (pair + 1) * PAIR_F)
-            inverse = acts.tile([P, HALF_TILES, PAIR_F], F32, name="inverse_o")
-            act_of[unit]["inverse_o"] = inverse
-            nc.scalar.activation(out=inverse[:], in_=sums_of[unit, "o"][:], func=ACT.Exp, scale=-1.0)
-            for tt in range(HALF_TILES):
-                nc.gpsimd.tensor_tensor(
-                    out=inverse[:, tt, :], in0=inverse[:, tt, :], in1=exp_minus_bo[:, feats], op=ALU.mult
-                )
-            nc.gpsimd.tensor_scalar(
-                out=inverse[:], in0=inverse[:], scalar1=1.0, scalar2=1.0, op0=ALU.add, op1=ALU.mult
+            halved_of[unit] = work.tile([P, HALF_TILES, PAIR_F], F32, name="halved")
+            nc.vector.scalar_tensor_tensor(
+                out=halved_of[unit][:], in0=sums_of[unit, "o"][:], scalar=0.5,
+                in1=half_bo[:, feats].unsqueeze(1).to_broadcast([P, HALF_TILES, PAIR_F]),
+                op0=ALU.mult, op1=ALU.add,
             )
+
+        def activate_output(unit):
+            act_of[unit]["o"] = acts.tile([P, HALF_TILES, PAIR_F], F32, name="act_o")
+            nc.scalar.activation(out=act_of[unit]["o"][:], in_=halved_of[unit][:], func=ACT.Tanh)
 
         def turn(unit):
             turned_of[unit] = {}
@@ -345,10 +345,10 @@ def tile_slstmcell_kernel(
                         out=new_n[half][:, :, feats], in0=twice["fn"][:], scalar=0.5, in1=turned["i"][:],
                         op0=ALU.mult, op1=ALU.add,
                     )
-                if step == "d":
+                if step == "oc":
                     nc.vector.scalar_tensor_tensor(
-                        out=recip[half][:, :, feats], in0=new_n[half][:, :, feats], scalar=DIV_EPS,
-                        in1=act_of[unit]["inverse_o"][:], op0=ALU.add, op1=ALU.mult,
+                        out=hidden[half][:, :, feats], in0=act_of[unit]["o"][:], scalar=1.0, in1=c_here,
+                        op0=ALU.add, op1=ALU.mult,
                     )
 
         def store_state(half, part):
@@ -361,7 +361,9 @@ def tile_slstmcell_kernel(
         def square_divisor(unit):
             pair, half = divmod(unit, HALVES)
             feats = slice(pair * PAIR_F, (pair + 1) * PAIR_F)
-            nc.scalar.activation(out=recip[half][:, :, feats], in_=recip[half][:, :, feats], func=ACT.Square)
+            nc.scalar.activation(
+                out=recip[half][:, :, feats], in_=new_n[half][:, :, feats], func=ACT.Square, bias=div_eps[:, 0:1]
+            )
 
         def reciprocal(squares):
             nc.scalar.activation(out=squares, in_=squares, func=ACT.Abs_reciprocal_sqrt)
@@ -372,7 +374,7 @@ def tile_slstmcell_kernel(
         def divide_and_sum(half, tt):
             total[half, tt] = small.tile([P, 1], F32, name="total")
             nc.vector.scalar_tensor_tensor(
-                out=hidden[half][:, tt, :], in0=new_c[half][:, tt, :], scalar=1.0, in1=recip[half][:, tt, :],
+                out=hidden[half][:, tt, :], in0=hidden[half][:, tt, :], scalar=1.0, in1=recip[half][:, tt, :],
                 op0=ALU.mult, op1=ALU.mult,
                 accum_out=total[half, tt][:],
             )
@@ -460,17 +462,14 @@ def tile_slstmcell_kernel(
             if unit == 0:
                 spread_output_bias()
                 mx_passes(0, "o")
-                activate_output(0)
                 mx_passes(1, "i")
                 activate(1, "i")
             if last:
-                update(unit, ("fn", "fc"))
-                update(unit - 1, ("d",))
-                square_divisor(unit - 1)
                 reciprocal(recip[0][:, 0, late])
-                reciprocal(recip[0][:, 1, early])
-                reciprocal(recip[0][:, 1, late])
-                update(unit, ("c", "n", "fm", "d"))
+                reciprocal(recip[0][:, 1, :])
+                update(unit, ("fn", "fc"))
+                update(unit - 1, ("oc",))
+                update(unit, ("n", "c", "fm", "oc"))
                 magnitude(unit)
                 square_divisor(unit)
                 divide_and_sum(0, 0)
@@ -480,16 +479,24 @@ def tile_slstmcell_kernel(
                     mx_passes(unit + 1, gate)
                     activate(unit + 1, gate)
                 mx_passes(unit + 1, "o")
-                activate_output(unit + 1)
                 update(unit, ("fn", "fc", "fm"))
                 if unit > 0:
-                    update(unit - 1, ("d",))
-                update(unit, ("n", "c", "m"))
+                    update(unit - 1, ("oc",))
+                update(unit, ("n", "c"))
+                if unit == 0:
+                    add_output_bias(0)
+                    activate_output(0)
+                add_output_bias(unit + 1)
+                update(unit, ("m",))
+                if unit > 0:
+                    square_divisor(unit - 1)
             if unit + 2 < UNITS:
                 mx_passes(unit + 2, "i")
                 activate(unit + 2, "i")
-            if 0 < unit < UNITS - 1:
-                square_divisor(unit - 1)
+            if not last:
+                activate_output(unit + 1)
+            if unit == UNITS - 2:
+                square_divisor(unit)
             if pair % 2 == 1:
                 store_state(half, pair // 2)
 

@@ -95,8 +95,6 @@ def tile_slstmcell_kernel(
         nc.gpsimd.tensor_copy(out=ident_bf16[:], in_=ident[:])
         bo_row = keep.tile([P, H], BF16)
         nc.gpsimd.memset(bo_row[:], 0.0)
-        beta_row = keep.tile([P, H], BF16)
-        nc.gpsimd.memset(beta_row[:], 0.0)
         ones = keep.tile([P, P], BF16)
         nc.gpsimd.memset(ones[:], 1.0)
         planes = {}
@@ -173,7 +171,6 @@ def tile_slstmcell_kernel(
                 load_old_state(1, 1)
         nc.sync.dma_start(out=gamma_all[:], in_=ln_gamma.partition_broadcast(P))
         nc.sync.dma_start(out=beta_all[:], in_=ln_beta.partition_broadcast(P))
-        nc.sync.dma_start(out=beta_row[0:1, :], in_=ln_beta.rearrange("(r f) -> r f", r=1))
 
         grouped = {}
 
@@ -369,7 +366,7 @@ def tile_slstmcell_kernel(
             nc.scalar.activation(out=squares, in_=squares, func=ACT.Abs_reciprocal_sqrt)
 
         squares = keep.tile([P, H], BF16)
-        total, minus_mean, sum_sq, rstd, diagonal, scaled_of = {}, {}, {}, {}, {}, {}
+        total, minus_mean, sum_sq, rstd = {}, {}, {}, {}
 
         def divide_and_sum(half, tt):
             total[half, tt] = small.tile([P, 1], F32, name="total")
@@ -412,30 +409,6 @@ def tile_slstmcell_kernel(
                 )
                 nc.sync.dma_start(
                     out=by_row_tile(out_0)[:, half * HALF_TILES + tt, cols], in_=recip[half][:, tt, cols]
-                )
-
-        def deviation_on_diagonal(half, tt):
-            diagonal[half, tt] = small.tile([P, P], F32, name="diagonal")
-            nc.scalar.activation(
-                out=diagonal[half, tt][:], in_=ident[:], func=ACT.Copy, scale=rstd[half, tt][:, 0:1]
-            )
-
-        def scale_on_tensor(half, tt):
-            for c in range(H // BANK):
-                cols = slice(c * BANK, (c + 1) * BANK)
-                scaled = gate_psum.tile([P, BANK], F32, name="scaled", tag="sums")
-                scaled_of[half, tt, c] = scaled
-                nc.tensor.matmul(scaled[:], lhsT=ones[:], rhs=beta_row[:, cols], start=True, stop=False)
-                nc.tensor.matmul(
-                    scaled[:], lhsT=diagonal[half, tt][:], rhs=recip[half][:, tt, cols], start=False, stop=True
-                )
-
-        def store_scaled(half, tt):
-            for c in range(H // BANK):
-                cols = slice(c * BANK, (c + 1) * BANK)
-                nc.scalar.copy(out=hidden[half][:, tt, cols], in_=scaled_of[half, tt, c][:])
-                nc.scalar.dma_start(
-                    out=by_row_tile(out_0)[:, half * HALF_TILES + tt, cols], in_=hidden[half][:, tt, cols]
                 )
 
         turn_combined(0, (nc.vector.tensor_copy, nc.scalar.copy, nc.vector.tensor_copy))
@@ -506,24 +479,22 @@ def tile_slstmcell_kernel(
         negative_mean(0, 1)
         inverse_deviation(0, 0)
         squared_deviations(0, 1)
-        deviation_on_diagonal(0, 0)
         inverse_deviation(0, 1)
-        reciprocal(recip[1][:, 0, :])
-        deviation_on_diagonal(0, 1)
-        reciprocal(recip[1][:, 1, :])
+        for tt in range(HALF_TILES):
+            reciprocal(recip[1][:, tt, :])
         for tt in range(HALF_TILES):
             centre(0, tt)
-            scale_on_tensor(0, tt)
+        for tt in range(HALF_TILES):
+            scale_and_store(0, tt)
         divide_and_sum(1, 0)
         negative_mean(1, 0)
         squared_deviations(1, 0)
         divide_and_sum(1, 1)
         negative_mean(1, 1)
         inverse_deviation(1, 0)
-        store_scaled(0, 0)
         squared_deviations(1, 1)
         inverse_deviation(1, 1)
-        store_scaled(0, 1)
         for tt in range(HALF_TILES):
             centre(1, tt)
+        for tt in range(HALF_TILES):
             scale_and_store(1, tt)

@@ -148,20 +148,20 @@ def tile_slstmcell_kernel(
             nc.sync.dma_start(out=old_c[:, rows, feats], in_=by_row_tile(c_prev)[:, rows, feats])
             nc.sync.dma_start(out=old_m[:, rows, feats], in_=by_row_tile(m_prev)[:, rows, feats])
 
+        load_combined(0)
         for a, name in enumerate(BIAS_ORDER):
-            nc.sync.dma_start(
+            nc.scalar.dma_start(
                 out=bias_rows[BLOCKS * a : BLOCKS * (a + 1), :],
                 in_=bias_in[name].rearrange("(j f) -> j f", f=P),
             )
-        load_combined(0)
-        for gate in ("i", "z", "f"):
-            load_weight_columns(0, gate)
-            load_scales(gate)
+        nc.scalar.dma_start(out=bo_row[0:1, :], in_=bo.rearrange("(r f) -> r f", r=1))
         load_combined(1)
+        for gate in ("i", "z", "f"):
+            load_scales(gate)
+            load_weight_columns(0, gate)
         load_old_state(0, 0)
-        load_weight_columns(0, "o")
         load_scales("o")
-        nc.sync.dma_start(out=bo_row[0:1, :], in_=bo.rearrange("(r f) -> r f", r=1))
+        load_weight_columns(0, "o")
         load_old_state(1, 0)
         for pair in range(1, PAIRS):
             for gate in GATES:
@@ -413,14 +413,12 @@ def tile_slstmcell_kernel(
 
         turn_combined(0, (nc.vector.tensor_copy, nc.scalar.copy, nc.vector.tensor_copy))
         quantise_combined(0)
-        turn_biases()
-        mx_passes(0, "i")
-        activate(0, "i")
-        for gate in ("z", "f"):
-            mx_passes(0, gate)
-            activate(0, gate)
         turn_combined(1, (nc.vector.tensor_copy,) * PASSES)
         quantise_combined(1)
+        turn_biases()
+        for gate in ("i", "z", "f"):
+            mx_passes(0, gate)
+            activate(0, gate)
         early, late = slice(0, H - PAIR_F), slice(H - PAIR_F, H)
         for unit in range(UNITS):
             pair, half = divmod(unit, HALVES)
@@ -432,11 +430,6 @@ def tile_slstmcell_kernel(
                 reciprocal(recip[0][:, 0, early])
             else:
                 magnitude(unit)
-            if unit == 0:
-                spread_output_bias()
-                mx_passes(0, "o")
-                mx_passes(1, "i")
-                activate(1, "i")
             if last:
                 reciprocal(recip[0][:, 0, late])
                 reciprocal(recip[0][:, 1, :])
@@ -448,18 +441,17 @@ def tile_slstmcell_kernel(
                 divide_and_sum(0, 0)
                 update(unit, ("m",))
             else:
-                for gate in ("z", "f"):
+                for gate in ("i", "z", "f") if unit == 0 else ("z", "f"):
                     mx_passes(unit + 1, gate)
                     activate(unit + 1, gate)
-                mx_passes(unit + 1, "o")
+                if unit == 0:
+                    spread_output_bias()
+                mx_passes(unit, "o")
                 update(unit, ("fn", "fc", "fm"))
                 if unit > 0:
                     update(unit - 1, ("oc",))
                 update(unit, ("n", "c"))
-                if unit == 0:
-                    add_output_bias(0)
-                    activate_output(0)
-                add_output_bias(unit + 1)
+                add_output_bias(unit)
                 update(unit, ("m",))
                 if unit > 0:
                     square_divisor(unit - 1)
@@ -467,8 +459,11 @@ def tile_slstmcell_kernel(
                 mx_passes(unit + 2, "i")
                 activate(unit + 2, "i")
             if not last:
-                activate_output(unit + 1)
+                activate_output(unit)
             if unit == UNITS - 2:
+                mx_passes(unit + 1, "o")
+                add_output_bias(unit + 1)
+                activate_output(unit + 1)
                 square_divisor(unit)
             if pair % 2 == 1:
                 store_state(half, pair // 2)

@@ -82,6 +82,7 @@ def tile_slstmcell_kernel(
         stage = ctx.enter_context(tc.tile_pool(name="stage", bufs=PASSES))
         acts = ctx.enter_context(tc.tile_pool(name="acts", bufs=2))
         work = ctx.enter_context(tc.tile_pool(name="work", bufs=2))
+        outputs = ctx.enter_context(tc.tile_pool(name="outputs", bufs=4))
         halves = ctx.enter_context(tc.tile_pool(name="halves", bufs=HALVES))
         quarters = ctx.enter_context(tc.tile_pool(name="quarters", bufs=3))
         products = ctx.enter_context(tc.tile_pool(name="products", bufs=1))
@@ -148,17 +149,25 @@ def tile_slstmcell_kernel(
             nc.sync.dma_start(out=old_c[:, rows, feats], in_=by_row_tile(c_prev)[:, rows, feats])
             nc.sync.dma_start(out=old_m[:, rows, feats], in_=by_row_tile(m_prev)[:, rows, feats])
 
-        load_combined(0)
-        for a, name in enumerate(BIAS_ORDER):
+        def load_bias(name):
+            a = BIAS_ORDER.index(name)
             nc.scalar.dma_start(
                 out=bias_rows[BLOCKS * a : BLOCKS * (a + 1), :],
                 in_=bias_in[name].rearrange("(j f) -> j f", f=P),
             )
-        nc.scalar.dma_start(out=bo_row[0:1, :], in_=bo.rearrange("(r f) -> r f", r=1))
+
+        load_combined(0)
+        load_bias("i")
+        load_bias("z")
+        load_bias("f")
         load_combined(1)
-        for gate in ("i", "z", "f"):
-            load_scales(gate)
-            load_weight_columns(0, gate)
+        load_scales("i")
+        load_weight_columns(0, "i")
+        load_scales("z")
+        load_weight_columns(0, "z")
+        load_scales("f")
+        load_weight_columns(0, "f")
+        nc.sync.dma_start(out=bo_row[0:1, :], in_=bo.rearrange("(r f) -> r f", r=1))
         load_old_state(0, 0)
         load_scales("o")
         load_weight_columns(0, "o")
@@ -226,7 +235,7 @@ def tile_slstmcell_kernel(
             hidden[half] = halves.tile([P, HALF_TILES, H], F32, name="hidden")
             recip[half] = halves.tile([P, HALF_TILES, H], F32, name="recip")
         new_m = {}
-        sums_of, act_of, turned_of, size_of, twice_of, halved_of = {}, {}, {}, {}, {}, {}
+        sums_of, act_of, turned_of, size_of, twice_of, output_of = {}, {}, {}, {}, {}, {}
 
         def mx_passes(unit, gate):
             pair, half = divmod(unit, HALVES)
@@ -277,16 +286,15 @@ def tile_slstmcell_kernel(
         def add_output_bias(unit):
             pair = unit // HALVES
             feats = slice(pair * PAIR_F, (pair + 1) * PAIR_F)
-            halved_of[unit] = work.tile([P, HALF_TILES, PAIR_F], F32, name="halved")
+            output_of[unit] = outputs.tile([P, HALF_TILES, PAIR_F], F32, name="output")
             nc.vector.scalar_tensor_tensor(
-                out=halved_of[unit][:], in0=sums_of[unit, "o"][:], scalar=0.5,
+                out=output_of[unit][:], in0=sums_of[unit, "o"][:], scalar=0.5,
                 in1=half_bo[:, feats].unsqueeze(1).to_broadcast([P, HALF_TILES, PAIR_F]),
                 op0=ALU.mult, op1=ALU.add,
             )
 
         def activate_output(unit):
-            act_of[unit]["o"] = acts.tile([P, HALF_TILES, PAIR_F], F32, name="act_o")
-            nc.scalar.activation(out=act_of[unit]["o"][:], in_=halved_of[unit][:], func=ACT.Tanh)
+            nc.scalar.activation(out=output_of[unit][:], in_=output_of[unit][:], func=ACT.Tanh)
 
         def turn(unit):
             turned_of[unit] = {}
@@ -344,7 +352,7 @@ def tile_slstmcell_kernel(
                     )
                 if step == "oc":
                     nc.vector.scalar_tensor_tensor(
-                        out=hidden[half][:, :, feats], in0=act_of[unit]["o"][:], scalar=1.0, in1=c_here,
+                        out=hidden[half][:, :, feats], in0=output_of[unit][:], scalar=1.0, in1=c_here,
                         op0=ALU.add, op1=ALU.mult,
                     )
 
@@ -416,55 +424,51 @@ def tile_slstmcell_kernel(
         turn_combined(1, (nc.vector.tensor_copy,) * PASSES)
         quantise_combined(1)
         turn_biases()
-        for gate in ("i", "z", "f"):
-            mx_passes(0, gate)
-            activate(0, gate)
-        early, late = slice(0, H - PAIR_F), slice(H - PAIR_F, H)
+        mx_passes(0, "i")
+        activate(0, "i")
+        mx_passes(0, "z")
+        activate(0, "z")
+        mx_passes(0, "f")
+        activate(0, "f")
+        outputs_in = {0: (0,), 1: (1, 2), 2: (3, 4), 3: (5,), 4: (6,), 5: (7,), 6: ()}
+        hidden_in = {0: (), 1: (0,), 2: (1, 2)}
         for unit in range(UNITS):
             pair, half = divmod(unit, HALVES)
             last = unit == UNITS - 1
             turn(unit)
             if last:
+                square_divisor(unit - 1)
                 scratch = small.tile([P, 1], F32)
                 nc.scalar.activation(out=scratch[:], in_=ln_eps[:], func=ACT.Abs_reciprocal_sqrt)
-                reciprocal(recip[0][:, 0, early])
-            else:
-                magnitude(unit)
-            if last:
-                reciprocal(recip[0][:, 0, late])
-                reciprocal(recip[0][:, 1, :])
-                update(unit, ("fn", "fc"))
-                update(unit - 1, ("oc",))
-                update(unit, ("n", "c", "fm", "oc"))
+                for tt in range(HALF_TILES):
+                    reciprocal(recip[0][:, tt, :])
+                update(unit, ("fn", "fc", "n", "fm", "c"))
                 magnitude(unit)
                 square_divisor(unit)
                 divide_and_sum(0, 0)
-                update(unit, ("m",))
+                update(unit, ("oc", "m"))
             else:
+                magnitude(unit)
                 for gate in ("i", "z", "f") if unit == 0 else ("z", "f"):
                     mx_passes(unit + 1, gate)
                     activate(unit + 1, gate)
                 if unit == 0:
                     spread_output_bias()
-                mx_passes(unit, "o")
-                update(unit, ("fn", "fc", "fm"))
-                if unit > 0:
-                    update(unit - 1, ("oc",))
-                update(unit, ("n", "c"))
-                add_output_bias(unit)
+                for ready in outputs_in[unit]:
+                    mx_passes(ready, "o")
+                update(unit, ("fn", "fc", "fm", "n", "c"))
+                for ready in outputs_in[unit]:
+                    add_output_bias(ready)
+                for ready in hidden_in.get(unit, (unit,)):
+                    update(ready, ("oc",))
                 update(unit, ("m",))
                 if unit > 0:
                     square_divisor(unit - 1)
-            if unit + 2 < UNITS:
-                mx_passes(unit + 2, "i")
-                activate(unit + 2, "i")
-            if not last:
-                activate_output(unit)
-            if unit == UNITS - 2:
-                mx_passes(unit + 1, "o")
-                add_output_bias(unit + 1)
-                activate_output(unit + 1)
-                square_divisor(unit)
+                if unit + 2 < UNITS:
+                    mx_passes(unit + 2, "i")
+                    activate(unit + 2, "i")
+                for ready in outputs_in[unit]:
+                    activate_output(ready)
             if pair % 2 == 1:
                 store_state(half, pair // 2)
 

@@ -428,28 +428,35 @@ def tile_slstmcell_kernel(
         activate(0, "i")
         mx_passes(0, "z")
         activate(0, "z")
+        mx_passes(1, "i")
+        activate(1, "i")
         mx_passes(0, "f")
         activate(0, "f")
-        outputs_in = {0: (0,), 1: (1, 2), 2: (3, 4), 3: (5,), 4: (6,), 5: (7,), 6: ()}
-        hidden_in = {0: (), 1: (0,), 2: (1, 2)}
+        mx_passes(1, "z")
+        activate(1, "z")
+        early = slice(0, H - PAIR_F)
+        late = slice(H - PAIR_F, H)
+        outputs_in = {0: (0,), 1: (1,), 2: (2, 3), 3: (4,), 4: (5, 6), 5: (7,), 6: ()}
+        hidden_in = {0: (), 1: (0,), 2: (1,), 3: (2, 3)}
         for unit in range(UNITS):
             pair, half = divmod(unit, HALVES)
             last = unit == UNITS - 1
             turn(unit)
             if last:
-                square_divisor(unit - 1)
                 scratch = small.tile([P, 1], F32)
                 nc.scalar.activation(out=scratch[:], in_=ln_eps[:], func=ACT.Abs_reciprocal_sqrt)
-                for tt in range(HALF_TILES):
-                    reciprocal(recip[0][:, tt, :])
+                reciprocal(recip[0][:, 0, early])
+                square_divisor(unit - 1)
+                reciprocal(recip[0][:, 0, late])
+                reciprocal(recip[0][:, 1, :])
                 update(unit, ("fn", "fc", "n", "fm", "c"))
                 magnitude(unit)
-                square_divisor(unit)
                 divide_and_sum(0, 0)
                 update(unit, ("oc", "m"))
+                square_divisor(unit)
             else:
                 magnitude(unit)
-                for gate in ("i", "z", "f") if unit == 0 else ("z", "f"):
+                for gate in {0: ("f",), 1: ("i", "z", "f")}.get(unit, ("z", "f")):
                     mx_passes(unit + 1, gate)
                     activate(unit + 1, gate)
                 if unit == 0:
@@ -464,7 +471,7 @@ def tile_slstmcell_kernel(
                 update(unit, ("m",))
                 if unit > 0:
                     square_divisor(unit - 1)
-                if unit + 2 < UNITS:
+                if 0 < unit < UNITS - 2:
                     mx_passes(unit + 2, "i")
                     activate(unit + 2, "i")
                 for ready in outputs_in[unit]:
@@ -479,12 +486,12 @@ def tile_slstmcell_kernel(
         inverse_deviation(0, 0)
         squared_deviations(0, 1)
         inverse_deviation(0, 1)
-        for tt in range(HALF_TILES):
-            reciprocal(recip[1][:, tt, :])
-        for tt in range(HALF_TILES):
-            centre(0, tt)
-        for tt in range(HALF_TILES):
-            scale_and_store(0, tt)
+        reciprocal(recip[1][:, 0, :])
+        reciprocal(recip[1][:, 1, :])
+        centre(0, 0)
+        centre(0, 1)
+        scale_and_store(0, 0)
+        scale_and_store(0, 1)
         divide_and_sum(1, 0)
         negative_mean(1, 0)
         squared_deviations(1, 0)
@@ -493,7 +500,7 @@ def tile_slstmcell_kernel(
         inverse_deviation(1, 0)
         squared_deviations(1, 1)
         inverse_deviation(1, 1)
-        for tt in range(HALF_TILES):
-            centre(1, tt)
-        for tt in range(HALF_TILES):
-            scale_and_store(1, tt)
+        centre(1, 0)
+        centre(1, 1)
+        scale_and_store(1, 0)
+        scale_and_store(1, 1)

@@ -84,7 +84,7 @@ def tile_slstmcell_kernel(
         work = ctx.enter_context(tc.tile_pool(name="work", bufs=2))
         outputs = ctx.enter_context(tc.tile_pool(name="outputs", bufs=4))
         halves = ctx.enter_context(tc.tile_pool(name="halves", bufs=HALVES))
-        quarters = ctx.enter_context(tc.tile_pool(name="quarters", bufs=3))
+        quarters = ctx.enter_context(tc.tile_pool(name="quarters", bufs=2 * HALVES))
         products = ctx.enter_context(tc.tile_pool(name="products", bufs=1))
         small = ctx.enter_context(tc.tile_pool(name="small", bufs=ROW_TILES))
 
@@ -98,6 +98,10 @@ def tile_slstmcell_kernel(
         nc.gpsimd.memset(bo_row[:], 0.0)
         ones = keep.tile([P, P], BF16)
         nc.gpsimd.memset(ones[:], 1.0)
+        affine_row = {}
+        for name in ("gamma", "beta"):
+            affine_row[name] = keep.tile([P, H], BF16, name="row_" + name)
+            nc.gpsimd.memset(affine_row[name][:], 0.0)
         planes = {}
         for gate in GATES:
             planes[gate] = keep.tile([P, PASSES, H], U8, name="planes_" + gate, align_bytes=64)
@@ -116,8 +120,6 @@ def tile_slstmcell_kernel(
         codes = keep.tile([P, PASSES, B], U32, align_bytes=64)
         code_scales = keep.tile([P, PASSES, B], U8, align_bytes=64)
         bias_cols = keep.tile([P, BLOCKS * len(BIAS_ORDER)], F32)
-        gamma_all = keep.tile([P, H], BF16)
-        beta_all = keep.tile([P, H], BF16)
         x_rows, h_rows = {}, {}
         for half in range(HALVES):
             x_rows[half] = keep.tile([P, HALF_TILES, IN], BF16, name="x_rows_%d" % half)
@@ -142,12 +144,11 @@ def tile_slstmcell_kernel(
                 in_=words_in[gate].rearrange("g p n t -> p g (n t)").bitcast(I32)[:, :, cols],
             )
 
-        def load_old_state(half, part):
-            rows = slice(half * HALF_TILES, (half + 1) * HALF_TILES)
-            feats = slice(part * PART_F, (part + 1) * PART_F)
-            nc.sync.dma_start(out=old_n[:, rows, feats], in_=by_row_tile(n_prev)[:, rows, feats])
-            nc.sync.dma_start(out=old_c[:, rows, feats], in_=by_row_tile(c_prev)[:, rows, feats])
-            nc.sync.dma_start(out=old_m[:, rows, feats], in_=by_row_tile(m_prev)[:, rows, feats])
+        def load_old_state(first, past):
+            feats = slice(first * PAIR_F, past * PAIR_F)
+            nc.sync.dma_start(out=old_n[:, :, feats], in_=by_row_tile(n_prev)[:, :, feats])
+            nc.sync.dma_start(out=old_c[:, :, feats], in_=by_row_tile(c_prev)[:, :, feats])
+            nc.sync.dma_start(out=old_m[:, :, feats], in_=by_row_tile(m_prev)[:, :, feats])
 
         def load_bias(name):
             a = BIAS_ORDER.index(name)
@@ -168,18 +169,18 @@ def tile_slstmcell_kernel(
         load_scales("f")
         load_weight_columns(0, "f")
         nc.sync.dma_start(out=bo_row[0:1, :], in_=bo.rearrange("(r f) -> r f", r=1))
-        load_old_state(0, 0)
+        load_old_state(0, 1)
         load_scales("o")
         load_weight_columns(0, "o")
-        load_old_state(1, 0)
         for pair in range(1, PAIRS):
-            for gate in GATES:
+            for gate in ("i", "z", "f", "o"):
                 load_weight_columns(pair, gate)
-            if pair == PAIRS // 2:
-                load_old_state(0, 1)
-                load_old_state(1, 1)
-        nc.sync.dma_start(out=gamma_all[:], in_=ln_gamma.partition_broadcast(P))
-        nc.sync.dma_start(out=beta_all[:], in_=ln_beta.partition_broadcast(P))
+            if pair == 1:
+                load_old_state(1, 2)
+            if pair == 2:
+                load_old_state(2, PAIRS)
+        for name, dram in (("gamma", ln_gamma), ("beta", ln_beta)):
+            nc.sync.dma_start(out=affine_row[name][0:1, :], in_=dram.rearrange("(r f) -> r f", r=1))
 
         grouped = {}
 
@@ -402,18 +403,30 @@ def tile_slstmcell_kernel(
                 bias=ln_eps[:, 0:1],
             )
 
+        chunks = [slice(c * BANK, (c + 1) * BANK) for c in range(H // BANK)]
+        affine_of = {}
+
+        def spread_affine():
+            for name in ("gamma", "beta"):
+                for c, cols in enumerate(chunks):
+                    affine_of[name, c] = gate_psum.tile([P, BANK], F32, name="affine", tag="sums")
+                    nc.tensor.matmul(
+                        affine_of[name, c][:], lhsT=ones[:], rhs=affine_row[name][:, cols], start=True, stop=True
+                    )
+
         def centre(half, tt):
-            nc.vector.scalar_tensor_tensor(
-                out=recip[half][:, tt, :], in0=hidden[half][:, tt, :], scalar=minus_mean[half, tt][:, 0:1],
-                in1=gamma_all[:], op0=ALU.add, op1=ALU.mult,
-            )
+            for c, cols in enumerate(chunks):
+                nc.vector.scalar_tensor_tensor(
+                    out=recip[half][:, tt, cols], in0=hidden[half][:, tt, cols],
+                    scalar=minus_mean[half, tt][:, 0:1], in1=affine_of["gamma", c][:],
+                    op0=ALU.add, op1=ALU.mult,
+                )
 
         def scale_and_store(half, tt):
-            for c in range(H // BANK):
-                cols = slice(c * BANK, (c + 1) * BANK)
+            for c, cols in enumerate(chunks):
                 nc.vector.scalar_tensor_tensor(
                     out=recip[half][:, tt, cols], in0=recip[half][:, tt, cols], scalar=rstd[half, tt][:, 0:1],
-                    in1=beta_all[:, cols], op0=ALU.mult, op1=ALU.add,
+                    in1=affine_of["beta", c][:], op0=ALU.mult, op1=ALU.add,
                 )
                 nc.sync.dma_start(
                     out=by_row_tile(out_0)[:, half * HALF_TILES + tt, cols], in_=recip[half][:, tt, cols]
@@ -436,8 +449,8 @@ def tile_slstmcell_kernel(
         activate(1, "z")
         early = slice(0, H - PAIR_F)
         late = slice(H - PAIR_F, H)
-        outputs_in = {0: (0,), 1: (1,), 2: (2, 3), 3: (4,), 4: (5, 6), 5: (7,), 6: ()}
-        hidden_in = {0: (), 1: (0,), 2: (1,), 3: (2, 3)}
+        outputs_in = {0: (0,), 1: (1,), 2: (2,), 3: (3, 4), 4: (5,), 5: (6, 7), 6: ()}
+        hidden_in = {0: (), 1: (0,), 2: (1,), 3: (2,), 4: (3, 4)}
         for unit in range(UNITS):
             pair, half = divmod(unit, HALVES)
             last = unit == UNITS - 1
@@ -479,6 +492,7 @@ def tile_slstmcell_kernel(
             if pair % 2 == 1:
                 store_state(half, pair // 2)
 
+        spread_affine()
         negative_mean(0, 0)
         squared_deviations(0, 0)
         divide_and_sum(0, 1)

from contextlib import ExitStack

import concourse.mybir as mybir
from concourse.masks import make_identity

F32 = mybir.dt.float32
BF16 = mybir.dt.bfloat16
I32 = mybir.dt.int32
U32 = mybir.dt.uint32
U8 = mybir.dt.uint8
FP8X4 = mybir.dt.float8_e4m3fn_x4
ACT = mybir.ActivationFunctionType
ALU = mybir.AluOpType

P = 128
B, IN, H = 512, 512, 1024
D = IN + H
K_PASS = 4 * P
PASSES = D // K_PASS
LN_EPS = 1e-5
DIV_EPS = 1e-6

ROW_TILES = B // P
HALVES = 2
HALF_TILES = ROW_TILES // HALVES
HALF_B = B // HALVES
PAIR_F = 2 * P
PAIRS = H // PAIR_F
UNITS = HALVES * PAIRS
PART_F = 2 * PAIR_F
BANK = 512
BLOCKS = H // P

GATES = ("i", "z", "f", "o")
BIAS_ORDER = ("i", "z", "f")
TURNED = ("f", "i", "iz")

FLOPS = 2 * B * D * 4 * H


def tile_slstmcell_kernel(
    tc,
    x,
    h_prev,
    c_prev,
    n_prev,
    m_prev,
    Wi_words,
    Wi_scales,
    bi,
    Wf_words,
    Wf_scales,
    bf,
    Wo_words,
    Wo_scales,
    bo,
    Wz_words,
    Wz_scales,
    bz,
    ln_gamma,
    ln_beta,
    out_0,
    out_1,
    out_2,
    out_3,
):
    nc = tc.nc
    words_in = {"i": Wi_words, "z": Wz_words, "f": Wf_words, "o": Wo_words}
    scales_in = {"i": Wi_scales, "z": Wz_scales, "f": Wf_scales, "o": Wo_scales}
    bias_in = {"i": bi, "z": bz, "f": bf, "o": bo}
    gate_func = {"i": ACT.Exp, "z": ACT.Tanh, "f": ACT.Tanh}
    gate_scale = {"i": 1.0, "z": 1.0, "f": 0.5}

    def by_row_tile(dram):
        return dram.rearrange("(t p) f -> p t f", p=P)

    with ExitStack() as ctx:
        ctx.enter_context(tc.manual_schedule())
        keep = ctx.enter_context(tc.tile_pool(name="keep", bufs=1))
        gate_psum = ctx.enter_context(tc.psum_pool(name="gate_psum", bufs=len(GATES)))
        turn_psum = ctx.enter_context(tc.psum_pool(name="turn_psum", bufs=4))
        stage = ctx.enter_context(tc.tile_pool(name="stage", bufs=PASSES))
        acts = ctx.enter_context(tc.tile_pool(name="acts", bufs=2))
        work = ctx.enter_context(tc.tile_pool(name="work", bufs=2))
        outputs = ctx.enter_context(tc.tile_pool(name="outputs", bufs=4))
        halves = ctx.enter_context(tc.tile_pool(name="halves", bufs=HALVES))
        quarters = ctx.enter_context(tc.tile_pool(name="quarters", bufs=2 * HALVES))
        products = ctx.enter_context(tc.tile_pool(name="products", bufs=1))
        small = ctx.enter_context(tc.tile_pool(name="small", bufs=ROW_TILES))

        bias_rows = keep.tile([P, P], BF16)
        nc.gpsimd.memset(bias_rows[:], 0.0)
        ident = keep.tile([P, P], F32)
        make_identity(nc, ident[:])
        ident_bf16 = keep.tile([P, P], BF16)
        nc.gpsimd.tensor_copy(out=ident_bf16[:], in_=ident[:])
        bo_row = keep.tile([P, H], BF16)
        nc.gpsimd.memset(bo_row[:], 0.0)
        ones = keep.tile([P, P], BF16)
        nc.gpsimd.memset(ones[:], 1.0)
        affine_row = {}
        for name in ("gamma", "beta"):
            affine_row[name] = keep.tile([P, H], BF16, name="row_" + name)
            nc.gpsimd.memset(affine_row[name][:], 0.0)
        planes = {}
        for gate in GATES:
            planes[gate] = keep.tile([P, PASSES, H], U8, name="planes_" + gate, align_bytes=64)
            nc.vector.memset(planes[gate][:].rearrange("p g n -> p (g n)").bitcast(I32), 0)
        div_eps = keep.tile([P, 1], F32)
        nc.vector.memset(div_eps[:], DIV_EPS)
        ln_eps = keep.tile([P, 1], F32)
        nc.vector.memset(ln_eps[:], 4.0 * LN_EPS)

        w_words = {}
        for gate in GATES:
            w_words[gate] = keep.tile([P, PASSES, H], U32, name="w_words_" + gate, align_bytes=64)
        old_n = keep.tile([P, ROW_TILES, H], BF16)
        old_c = keep.tile([P, ROW_TILES, H], BF16)
        old_m = keep.tile([P, ROW_TILES, H], BF16)
        codes = keep.tile([P, PASSES, B], U32, align_bytes=64)
        code_scales = keep.tile([P, PASSES, B], U8, align_bytes=64)
        bias_cols = keep.tile([P, BLOCKS * len(BIAS_ORDER)], F32)
        x_rows, h_rows = {}, {}
        for half in range(HALVES):
            x_rows[half] = keep.tile([P, HALF_TILES, IN], BF16, name="x_rows_%d" % half)
            h_rows[half] = keep.tile([P, HALF_TILES, H], BF16, name="h_rows_%d" % half)

        def load_combined(half):
            rows = slice(half * HALF_TILES, (half + 1) * HALF_TILES)
            nc.sync.dma_start(out=x_rows[half][:], in_=by_row_tile(x)[:, rows, :])
            nc.sync.dma_start(out=h_rows[half][:], in_=by_row_tile(h_prev)[:, rows, :])

        def load_scales(gate):
            for r in range(4):
                nc.sync.dma_start(
                    out=planes[gate][r : P : 32, :, :].bitcast(I32),
                    in_=scales_in[gate].rearrange("g (q r) n -> r q g n", r=4)[r].bitcast(I32),
                )

        def load_weight_columns(pair, gate):
            cols = slice(pair * PAIR_F, (pair + 1) * PAIR_F)
            nc.sync.dma_start(
                out=w_words[gate][:, :, cols].bitcast(I32),
                in_=words_in[gate].rearrange("g p n t -> p g (n t)").bitcast(I32)[:, :, cols],
            )

        def load_old_state(first, past):
            feats = slice(first * PAIR_F, past * PAIR_F)
            nc.sync.dma_start(out=old_n[:, :, feats], in_=by_row_tile(n_prev)[:, :, feats])
            nc.sync.dma_start(out=old_c[:, :, feats], in_=by_row_tile(c_prev)[:, :, feats])
            nc.sync.dma_start(out=old_m[:, :, feats], in_=by_row_tile(m_prev)[:, :, feats])

        def load_bias(name):
            a = BIAS_ORDER.index(name)
            nc.scalar.dma_start(
                out=bias_rows[BLOCKS * a : BLOCKS * (a + 1), :],
                in_=bias_in[name].rearrange("(j f) -> j f", f=P),
            )

        load_combined(0)
        load_bias("i")
        load_bias("z")
        load_bias("f")
        load_combined(1)
        load_scales("i")
        load_weight_columns(0, "i")
        load_scales("z")
        load_weight_columns(0, "z")
        load_scales("f")
        load_weight_columns(0, "f")
        nc.sync.dma_start(out=bo_row[0:1, :], in_=bo.rearrange("(r f) -> r f", r=1))
        load_old_state(0, 1)
        load_scales("o")
        load_weight_columns(0, "o")
        for pair in range(1, PAIRS):
            for gate in ("i", "z", "f", "o"):
                load_weight_columns(pair, gate)
            if pair == 1:
                load_old_state(1, 2)
            if pair == 2:
                load_old_state(2, PAIRS)
        for name, dram in (("gamma", ln_gamma), ("beta", ln_beta)):
            nc.sync.dma_start(out=affine_row[name][0:1, :], in_=dram.rearrange("(r f) -> r f", r=1))

        grouped = {}

        def turn_combined(half, copy_engines):
            for g in range(PASSES):
                k_turned = turn_psum.tile([P, 2, HALF_B], F32, tag="turn")
                for tt in range(HALF_TILES):
                    if g == 0:
                        pairs_of_k = x_rows[half][:, tt, :].bitcast(F32)
                    else:
                        pairs_of_k = h_rows[half][:, tt, :].bitcast(F32)[:, 256 * (g - 1) : 256 * g]
                    for u in range(2):
                        nc.tensor.transpose(
                            k_turned[:, u, tt * P : (tt + 1) * P],
                            pairs_of_k[:, u : 256 : 2],
                            ident[:],
                        )
                grouped[half, g] = stage.tile([P, HALF_B, 4], BF16, name="grouped", align_bytes=64)
                copy_engines[g](
                    out=grouped[half, g][:].bitcast(F32),
                    in_=k_turned[:].rearrange("p u b -> p b u"),
                )

        def quantise_combined(half):
            for g in range(PASSES):
                rows = slice(half * HALF_B, (half + 1) * HALF_B)
                nc.vector.quantize_mx(
                    out=codes[:, g, rows].bitcast(FP8X4),
                    scales=code_scales[:, g, rows],
                    in_=grouped[half, g][:].rearrange("p b t -> p (b t)"),
                )

        half_bo = keep.tile([P, H], BF16)

        def turn_biases():
            bias_turned = turn_psum.tile([P, P], BF16, tag="turn")
            nc.tensor.transpose(bias_turned[:], bias_rows[:], ident_bf16[:])
            whole = BLOCKS * BIAS_ORDER.index("f")
            nc.scalar.copy(out=bias_cols[:, 0:whole], in_=bias_turned[:, 0:whole])
            nc.scalar.mul(out=bias_cols[:, whole:], in_=bias_turned[:, whole : BLOCKS * len(BIAS_ORDER)], mul=0.5)

        def spread_output_bias():
            for c in range(H // BANK):
                cols = slice(c * BANK, (c + 1) * BANK)
                spread = gate_psum.tile([P, BANK], F32, tag="sums")
                nc.tensor.matmul(spread[:], lhsT=ones[:], rhs=bo_row[:, cols], start=True, stop=True)
                nc.scalar.mul(out=half_bo[:, cols], in_=spread[:], mul=0.5)

        new_n, new_c, hidden, recip = {}, {}, {}, {}
        for half in range(HALVES):
            new_c[half] = halves.tile([P, HALF_TILES, H], F32, name="new_c")
            new_n[half] = halves.tile([P, HALF_TILES, H], F32, name="new_n")
            hidden[half] = halves.tile([P, HALF_TILES, H], F32, name="hidden")
            recip[half] = halves.tile([P, HALF_TILES, H], F32, name="recip")
        new_m = {}
        sums_of, act_of, turned_of, size_of, twice_of, output_of = {}, {}, {}, {}, {}, {}

        def mx_passes(unit, gate):
            pair, half = divmod(unit, HALVES)
            sums = gate_psum.tile([P, 2, HALF_B], F32, tag="sums")
            sums_of[unit, gate] = sums
            for s in range(2):
                if gate == "o":
                    tile_rows = slice((half * HALF_TILES + s) * P, (half * HALF_TILES + s + 1) * P)
                    feats = slice(pair * PAIR_F, (pair + 1) * PAIR_F)
                    still, still_scale, still_cols = codes, code_scales, tile_rows
                    moving, moving_scale, moving_cols = w_words[gate], planes[gate], feats
                else:
                    feats = slice((2 * pair + s) * P, (2 * pair + s + 1) * P)
                    rows = slice(half * HALF_B, (half + 1) * HALF_B)
                    still, still_scale, still_cols = w_words[gate], planes[gate], feats
                    moving, moving_scale, moving_cols = codes, code_scales, rows
                for g in range(PASSES):
                    nc.tensor.matmul_mx(
                        out=sums[:, s, :],
                        lhsT=still[:, g, still_cols].bitcast(FP8X4),
                        lhsT_scale=still_scale[:, g, still_cols],
                        rhs=moving[:, g, moving_cols].bitcast(FP8X4),
                        rhs_scale=moving_scale[:, g, moving_cols],
                        start=(g == 0),
                        stop=(g == PASSES - 1),
                    )

        def activate(unit, gate):
            pair = unit // HALVES
            act = act_of.setdefault(unit, {})
            act[gate] = acts.tile([P, 2, HALF_B], F32, name="act_" + gate)
            if gate == "z":
                act["iz"] = acts.tile([P, 2, HALF_B], F32, name="act_iz")
            for s in range(2):
                col = BLOCKS * BIAS_ORDER.index(gate) + 2 * pair + s
                nc.scalar.activation(
                    out=act[gate][:, s, :],
                    in_=sums_of[unit, gate][:, s, :],
                    func=gate_func[gate],
                    bias=bias_cols[:, col : col + 1],
                    scale=gate_scale[gate],
                )
                if gate == "z":
                    nc.gpsimd.tensor_tensor(
                        out=act["iz"][:, s, :], in0=act["i"][:, s, :], in1=act["z"][:, s, :], op=ALU.mult
                    )

        def add_output_bias(unit):
            pair = unit // HALVES
            feats = slice(pair * PAIR_F, (pair + 1) * PAIR_F)
            output_of[unit] = outputs.tile([P, HALF_TILES, PAIR_F], F32, name="output")
            nc.vector.scalar_tensor_tensor(
                out=output_of[unit][:], in0=sums_of[unit, "o"][:], scalar=0.5,
                in1=half_bo[:, feats].unsqueeze(1).to_broadcast([P, HALF_TILES, PAIR_F]),
                op0=ALU.mult, op1=ALU.add,
            )

        def activate_output(unit):
            nc.scalar.activation(out=output_of[unit][:], in_=output_of[unit][:], func=ACT.Tanh)

        def turn(unit):
            turned_of[unit] = {}
            for name in TURNED:
                turned = turn_psum.tile([P, HALF_TILES, PAIR_F], F32, name="turned_" + name, tag="turn")
                turned_of[unit][name] = turned
                for s in range(2):
                    for tt in range(HALF_TILES):
                        nc.tensor.transpose(
                            turned[:, tt, s * P : (s + 1) * P],
                            act_of[unit][name][:, s, tt * P : (tt + 1) * P],
                            ident[:],
                        )

        def magnitude(unit):
            size_of[unit] = work.tile([P, HALF_TILES, PAIR_F], F32, name="size_iz")
            nc.scalar.activation(out=size_of[unit][:], in_=turned_of[unit]["iz"][:], func=ACT.Abs)

        def update(unit, steps):
            pair, half = divmod(unit, HALVES)
            part, side = divmod(pair, 2)
            turned = turned_of[unit]
            tiles = slice(half * HALF_TILES, (half + 1) * HALF_TILES)
            feats = slice(pair * PAIR_F, (pair + 1) * PAIR_F)
            in_part = slice(side * PAIR_F, (side + 1) * PAIR_F)
            old = {"fm": old_m, "fc": old_c, "fn": old_n}
            if unit not in twice_of:
                if side == 0:
                    new_m[half, part] = quarters.tile([P, HALF_TILES, PART_F], F32, name="new_m")
                twice_of[unit] = {}
                for name in ("fm", "fc", "fn"):
                    twice_of[unit][name] = products.tile([P, HALF_TILES, PAIR_F], F32, name="twice_" + name)
            twice = twice_of[unit]
            c_here = new_c[half][:, :, feats]
            for step in steps:
                if step in old:
                    nc.vector.scalar_tensor_tensor(
                        out=twice[step][:], in0=turned["f"][:], scalar=1.0, in1=old[step][:, tiles, feats],
                        op0=ALU.add, op1=ALU.mult,
                    )
                if step == "m":
                    nc.vector.scalar_tensor_tensor(
                        out=new_m[half, part][:, :, in_part], in0=twice["fm"][:], scalar=0.5,
                        in1=size_of[unit][:], op0=ALU.mult, op1=ALU.max,
                    )
                if step == "c":
                    nc.vector.scalar_tensor_tensor(
                        out=c_here, in0=twice["fc"][:], scalar=0.5, in1=turned["iz"][:],
                        op0=ALU.mult, op1=ALU.add,
                    )
                if step == "n":
                    nc.vector.scalar_tensor_tensor(
                        out=new_n[half][:, :, feats], in0=twice["fn"][:], scalar=0.5, in1=turned["i"][:],
                        op0=ALU.mult, op1=ALU.add,
                    )
                if step == "oc":
                    nc.vector.scalar_tensor_tensor(
                        out=hidden[half][:, :, feats], in0=output_of[unit][:], scalar=1.0, in1=c_here,
                        op0=ALU.add, op1=ALU.mult,
                    )

        def store_state(half, part):
            tiles = slice(half * HALF_TILES, (half + 1) * HALF_TILES)
            feats = slice(part * PART_F, (part + 1) * PART_F)
            nc.sync.dma_start(out=by_row_tile(out_3)[:, tiles, feats], in_=new_m[half, part][:])
            nc.sync.dma_start(out=by_row_tile(out_1)[:, tiles, feats], in_=new_c[half][:, :, feats])
            nc.sync.dma_start(out=by_row_tile(out_2)[:, tiles, feats], in_=new_n[half][:, :, feats])

        def square_divisor(unit):
            pair, half = divmod(unit, HALVES)
            feats = slice(pair * PAIR_F, (pair + 1) * PAIR_F)
            nc.scalar.activation(
                out=recip[half][:, :, feats], in_=new_n[half][:, :, feats], func=ACT.Square, bias=div_eps[:, 0:1]
            )

        def reciprocal(squares):
            nc.scalar.activation(out=squares, in_=squares, func=ACT.Abs_reciprocal_sqrt)

        squares = keep.tile([P, H], BF16)
        total, minus_mean, sum_sq, rstd = {}, {}, {}, {}

        def divide_and_sum(half, tt):
            total[half, tt] = small.tile([P, 1], F32, name="total")
            nc.vector.scalar_tensor_tensor(
                out=hidden[half][:, tt, :], in0=hidden[half][:, tt, :], scalar=1.0, in1=recip[half][:, tt, :],
                op0=ALU.mult, op1=ALU.mult,
                accum_out=total[half, tt][:],
            )

        def negative_mean(half, tt):
            minus_mean[half, tt] = small.tile([P, 1], F32, name="minus_mean")
            nc.scalar.mul(out=minus_mean[half, tt][:], in_=total[half, tt][:], mul=-1.0 / H)

        def squared_deviations(half, tt):
            sum_sq[half, tt] = small.tile([P, 1], F32, name="sum_sq")
            nc.scalar.activation(
                out=squares[:], in_=hidden[half][:, tt, :], func=ACT.Square,
                bias=minus_mean[half, tt][:, 0:1], accum_out=sum_sq[half, tt][:],
            )

        def inverse_deviation(half, tt):
            rstd[half, tt] = small.tile([P, 1], F32, name="rstd")
            nc.scalar.activation(
                out=rstd[half, tt][:], in_=sum_sq[half, tt][:], func=ACT.Abs_reciprocal_sqrt, scale=1.0 / H,
                bias=ln_eps[:, 0:1],
            )

        chunks = [slice(c * BANK, (c + 1) * BANK) for c in range(H // BANK)]
        affine_of = {}

        def spread_affine():
            for name in ("gamma", "beta"):
                for c, cols in enumerate(chunks):
                    affine_of[name, c] = gate_psum.tile([P, BANK], F32, name="affine", tag="sums")
                    nc.tensor.matmul(
                        affine_of[name, c][:], lhsT=ones[:], rhs=affine_row[name][:, cols], start=True, stop=True
                    )

        def centre(half, tt):
            for c, cols in enumerate(chunks):
                nc.vector.scalar_tensor_tensor(
                    out=recip[half][:, tt, cols], in0=hidden[half][:, tt, cols],
                    scalar=minus_mean[half, tt][:, 0:1], in1=affine_of["gamma", c][:],
                    op0=ALU.add, op1=ALU.mult,
                )

        def scale_and_store(half, tt):
            for c, cols in enumerate(chunks):
                nc.vector.scalar_tensor_tensor(
                    out=recip[half][:, tt, cols], in0=recip[half][:, tt, cols], scalar=rstd[half, tt][:, 0:1],
                    in1=affine_of["beta", c][:], op0=ALU.mult, op1=ALU.add,
                )
                nc.sync.dma_start(
                    out=by_row_tile(out_0)[:, half * HALF_TILES + tt, cols], in_=recip[half][:, tt, cols]
                )

        turn_combined(0, (nc.vector.tensor_copy, nc.scalar.copy, nc.vector.tensor_copy))
        quantise_combined(0)
        turn_combined(1, (nc.vector.tensor_copy,) * PASSES)
        quantise_combined(1)
        turn_biases()
        mx_passes(0, "i")
        activate(0, "i")
        mx_passes(0, "z")
        activate(0, "z")
        mx_passes(1, "i")
        activate(1, "i")
        mx_passes(0, "f")
        activate(0, "f")
        mx_passes(1, "z")
        activate(1, "z")
        early = slice(0, H - PAIR_F)
        late = slice(H - PAIR_F, H)
        outputs_in = {0: (0,), 1: (1,), 2: (2,), 3: (3, 4), 4: (5,), 5: (6, 7), 6: ()}
        hidden_in = {0: (), 1: (0,), 2: (1,), 3: (2,), 4: (3, 4)}
        for unit in range(UNITS):
            pair, half = divmod(unit, HALVES)
            last = unit == UNITS - 1
            turn(unit)
            if last:
                scratch = small.tile([P, 1], F32)
                nc.scalar.activation(out=scratch[:], in_=ln_eps[:], func=ACT.Abs_reciprocal_sqrt)
                reciprocal(recip[0][:, 0, early])
                square_divisor(unit - 1)
                reciprocal(recip[0][:, 0, late])
                reciprocal(recip[0][:, 1, :])
                update(unit, ("fn", "fc", "n", "fm", "c"))
                magnitude(unit)
                divide_and_sum(0, 0)
                update(unit, ("oc", "m"))
                square_divisor(unit)
            else:
                magnitude(unit)
                for gate in {0: ("f",), 1: ("i", "z", "f")}.get(unit, ("z", "f")):
                    mx_passes(unit + 1, gate)
                    activate(unit + 1, gate)
                if unit == 0:
                    spread_output_bias()
                for ready in outputs_in[unit]:
                    mx_passes(ready, "o")
                update(unit, ("fn", "fc", "fm", "n", "c"))
                for ready in outputs_in[unit]:
                    add_output_bias(ready)
                for ready in hidden_in.get(unit, (unit,)):
                    update(ready, ("oc",))
                update(unit, ("m",))
                if unit > 0:
                    square_divisor(unit - 1)
                if 0 < unit < UNITS - 2:
                    mx_passes(unit + 2, "i")
                    activate(unit + 2, "i")
                for ready in outputs_in[unit]:
                    activate_output(ready)
            if pair % 2 == 1:
                store_state(half, pair // 2)

        spread_affine()
        negative_mean(0, 0)
        squared_deviations(0, 0)
        divide_and_sum(0, 1)
        negative_mean(0, 1)
        inverse_deviation(0, 0)
        squared_deviations(0, 1)
        inverse_deviation(0, 1)
        reciprocal(recip[1][:, 0, :])
        reciprocal(recip[1][:, 1, :])
        centre(0, 0)
        centre(0, 1)
        scale_and_store(0, 0)
        scale_and_store(0, 1)
        divide_and_sum(1, 0)
        negative_mean(1, 0)
        squared_deviations(1, 0)
        divide_and_sum(1, 1)
        negative_mean(1, 1)
        inverse_deviation(1, 0)
        squared_deviations(1, 1)
        inverse_deviation(1, 1)
        centre(1, 0)
        centre(1, 1)
        scale_and_store(1, 0)
        scale_and_store(1, 1)
